import numpy as np
import ml_dtypes


def mxq(x, axis, fmt="e4m3"):
    dtype, down = {"e4m3": (ml_dtypes.float8_e4m3fn, 7), "e5m2": (ml_dtypes.float8_e5m2, 14)}[fmt]
    v = np.moveaxis(np.asarray(x, np.float32).astype(ml_dtypes.bfloat16).astype(np.float64), axis, -1)
    blocks = v.reshape(v.shape[:-1] + (-1, 32))
    amax = np.abs(blocks).max(-1, keepdims=True)
    byte = np.maximum(np.where(amax > 0, np.frexp(amax)[1] - 1 + 127, 0) - down, 1)
    scale = np.exp2(byte - 127.0)
    codes = (blocks / scale).astype(np.float32).astype(dtype).astype(np.float64)
    return np.moveaxis((codes * scale).reshape(v.shape), -1, axis)


WIDE = False


def mx_kscale(k):
    if not WIDE:
        return np.ones(k)
    levels = np.array([10, -10, 5, -5, 0])
    a = np.random.permutation(np.resize(levels, k // 512 * 4)).reshape(k // 512, 4)
    idx = np.arange(k)
    return np.exp2(a[idx // 512, idx % 128 // 32])


BF16 = ml_dtypes.bfloat16


def bf(x):
    return np.asarray(x, np.float32).astype(BF16)


def f64(x):
    return np.asarray(x).astype(np.float64)


E2M1 = np.array([0.0, 0.5, 1.0, 1.5, 2.0, 3.0, 4.0, 6.0, -0.0, -0.5, -1.0, -1.5, -2.0, -3.0, -4.0, -6.0])


def pack_weight(w, fmt):
    k, n = w.shape
    w = f64(bf(w)).reshape(k // 32, 32, n)
    amax = np.abs(w).max(1)
    if fmt == "e4m3":
        byte = np.frexp(amax)[1] - 1 + 127 - 7
    else:
        mant, ex = np.frexp(amax / 6.0)
        byte = np.where(mant > 0.5, ex, ex - 1) + 127
    byte = np.clip(np.where(amax > 0, byte, 1), 1, 254)
    scaled = (w * np.exp2(127.0 - byte)[:, None, :]).reshape(k, n).astype(np.float32)
    by_word = np.ascontiguousarray(scaled.reshape(k // 512, 128, 4, n).transpose(0, 1, 3, 2))
    if fmt == "e4m3":
        words = by_word.astype(ml_dtypes.float8_e4m3fn).view(np.uint8)
    else:
        c = by_word.astype(ml_dtypes.float4_e2m1fn).view(np.uint8) & 0xF
        words = c[..., 0::2] | (c[..., 1::2] << 4)
    return np.ascontiguousarray(words), np.ascontiguousarray(byte.astype(np.uint8).reshape(k // 512, 16, n))


def unpack_weight(words, scales, fmt):
    g, p, n, _ = words.shape
    if fmt == "e4m3":
        vals = np.ascontiguousarray(words).view(ml_dtypes.float8_e4m3fn).astype(np.float64)
    else:
        nib = np.empty((g, p, n, 4), np.uint8)
        nib[..., 0::2] = words & 0xF
        nib[..., 1::2] = words >> 4
        vals = E2M1[nib]
    vals = vals * np.repeat(np.exp2(scales.astype(np.float64) - 127.0), 8, axis=1)[..., None]
    return vals.transpose(0, 1, 3, 2).reshape(g * 512, n)


B, S, FIN, D, AF, F, H = 4, 1024, 128, 1024, 256, 4096, 16
MAX_TIMESCALE = 10000.0
MIN_TIMESCALE = 1.0
EPS = 1e-3


def timing_signal(length, channels):
    num_ts = channels // 2
    log_inc = np.log(MAX_TIMESCALE / MIN_TIMESCALE) / max(num_ts - 1, 1)
    inv_ts = MIN_TIMESCALE * np.exp(np.arange(num_ts) * -log_inc)
    scaled = np.arange(length)[:, None] * inv_ts[None, :]
    return np.concatenate([np.sin(scaled), np.cos(scaled)], axis=1)[None, :, :]


def layer_norm(v, gamma, beta):
    mu = v.mean(-1, keepdims=True)
    var = v.var(-1, keepdims=True)
    return (v - mu) / np.sqrt(var + EPS) * gamma + beta


def setup_inputs():
    r = np.random.standard_normal
    s = mx_kscale(D)
    x = bf(r((B, S, FIN)))
    W_emb = bf(r((FIN, D)) / np.sqrt(FIN))
    b_emb = bf(0.1 * r(D))
    g0 = bf((1.0 + 0.1 * r(D)) * s)
    beta0 = bf(0.1 * r(D) * s)
    Wq_words, Wq_scales = pack_weight(r((D, AF)) / np.sqrt(D) / s[:, None], "e4m3")
    bq = bf(0.1 * r(AF))
    Wk_words, Wk_scales = pack_weight(r((D, AF)) / np.sqrt(D) / s[:, None], "e4m3")
    bk = bf(0.1 * r(AF))
    Wv_words, Wv_scales = pack_weight(r((D, AF)) / np.sqrt(D) / s[:, None], "e4m3")
    bv = bf(0.1 * r(AF))
    return {"x": x,
            "W_emb": W_emb, "b_emb": b_emb,
            "g0": g0, "beta0": beta0,
            "Wq_words": Wq_words, "Wq_scales": Wq_scales, "bq": bq,
            "Wk_words": Wk_words, "Wk_scales": Wk_scales, "bk": bk,
            "Wv_words": Wv_words, "Wv_scales": Wv_scales, "bv": bv}


def reference(x, W_emb, b_emb, g0, beta0, Wq_words, Wq_scales, bq, Wk_words, Wk_scales, bk, Wv_words, Wv_scales, bv):
    h = np.maximum(f64(x) @ f64(W_emb) + f64(b_emb), 0.0)
    h = h + timing_signal(S, D)
    h = layer_norm(h, f64(g0), f64(beta0))
    hq = mxq(h, 2, "e4m3")
    q = (hq @ unpack_weight(Wq_words, Wq_scales, "e4m3")) + f64(bq)
    k = (hq @ unpack_weight(Wk_words, Wk_scales, "e4m3")) + f64(bk)
    v = (hq @ unpack_weight(Wv_words, Wv_scales, "e4m3")) + f64(bv)
    return q, k, v

@@ -1,0 +1,307 @@
+import math
+from contextlib import ExitStack
+
+import concourse.mybir as mybir
+from concourse.masks import make_identity
+
+F32 = mybir.dt.float32
+BF16 = mybir.dt.bfloat16
+I32 = mybir.dt.int32
+U32 = mybir.dt.uint32
+U8 = mybir.dt.uint8
+FP8X4 = mybir.dt.float8_e4m3fn_x4
+ALU = mybir.AluOpType
+ACT = mybir.ActivationFunctionType
+AX = mybir.AxisListType
+
+P = 128
+BATCH = 4
+SEQ = 1024
+FIN = 128
+D = 1024
+NOUT = 256
+N3 = 3 * NOUT
+PACK = 4
+PASSES = D // (P * PACK)
+BLOCKS = PASSES * PACK
+GROUPS = SEQ // P
+EPS = 1e-3
+ROUND_MAGIC = 12582912.0
+DECAY = math.exp(-math.log(10000.0) / 511.0)
+
+FLOPS = 2 * BATCH * SEQ * FIN * D + 2 * BATCH * SEQ * D * N3
+
+
+def tile_ffnn_encoder_pa_t_kernel(
+    tc,
+    x,
+    W_emb,
+    b_emb,
+    g0,
+    beta0,
+    Wq_words,
+    Wq_scales,
+    bq,
+    Wk_words,
+    Wk_scales,
+    bk,
+    Wv_words,
+    Wv_scales,
+    bv,
+    out_0,
+    out_1,
+    out_2,
+):
+    nc = tc.nc
+    with ExitStack() as stack:
+        keep = stack.enter_context(tc.tile_pool(name="keep", bufs=1))
+        phase = stack.enter_context(tc.tile_pool(name="phase", bufs=2))
+        rows = stack.enter_context(tc.tile_pool(name="rows", bufs=2))
+        small = stack.enter_context(tc.tile_pool(name="small", bufs=3))
+        cols = stack.enter_context(tc.tile_pool(name="cols", bufs=2))
+        results = stack.enter_context(tc.tile_pool(name="results", bufs=4))
+        psum_z = stack.enter_context(tc.psum_pool(name="psum_z", bufs=4))
+        psum_t = stack.enter_context(tc.psum_pool(name="psum_t", bufs=2))
+        psum_o = stack.enter_context(tc.psum_pool(name="psum_o", bufs=1))
+
+        x_sb = keep.tile([P, BATCH, GROUPS * FIN], BF16)
+        for b in range(BATCH):
+            nc.sync.dma_start(out=x_sb[:, b, :], in_=x[b].rearrange("(p a) f -> p (a f)", a=GROUPS))
+        w_raw = keep.tile([P, D], BF16)
+        nc.sync.dma_start(out=w_raw[:], in_=W_emb)
+        vec_bf = keep.tile([P, 3, 16], BF16)
+        for i, vec in enumerate((b_emb, g0, beta0)):
+            nc.sync.dma_start(
+                out=vec_bf[:, i, 0:BLOCKS].rearrange("p (g t) -> p g t", t=PACK),
+                in_=vec.rearrange("(g p t) -> p g t", g=PASSES, t=PACK),
+            )
+        w_codes = keep.tile([P, PASSES, N3], U32, align_bytes=64)
+        w_planes = keep.tile([P, PASSES, N3], U8, align_bytes=64)
+        nc.vector.memset(w_planes[:].rearrange("p g n -> p (g n)").bitcast(I32), 0)
+        weights = ((Wq_words, Wq_scales, bq), (Wk_words, Wk_scales, bk), (Wv_words, Wv_scales, bv))
+        for j, (words, scales, bias) in enumerate(weights):
+            n_cols = slice(j * NOUT, (j + 1) * NOUT)
+            nc.sync.dma_start(
+                out=w_codes[:, :, n_cols].bitcast(I32),
+                in_=words.rearrange("g p n t -> p g (n t)").bitcast(I32),
+            )
+        for j, (words, scales, bias) in enumerate(weights):
+            n_cols = slice(j * NOUT, (j + 1) * NOUT)
+            for quad in range(4):
+                nc.sync.dma_start(
+                    out=w_planes[32 * quad : 32 * quad + 4, :, n_cols].bitcast(I32),
+                    in_=scales.bitcast(I32)[:, 4 * quad : 4 * quad + 4, :].rearrange("g r n -> r g n"),
+                )
+        bias_bf = keep.tile([P, N3], BF16)
+        for j, (words, scales, bias) in enumerate(weights):
+            nc.sync.dma_start(out=bias_bf[:, j * NOUT : (j + 1) * NOUT], in_=bias.partition_broadcast(P))
+
+        ident_bf = keep.tile([P, P], BF16)
+        make_identity(nc, ident_bf[:])
+        ident_f = keep.tile([P, P], F32)
+        make_identity(nc, ident_f[:])
+        pos_i = keep.tile([P, GROUPS], I32)
+        nc.gpsimd.iota(pos_i[:], pattern=[[1, GROUPS]], base=0, channel_multiplier=GROUPS)
+        pos = keep.tile([P, GROUPS], F32)
+        nc.vector.tensor_copy(out=pos[:], in_=pos_i[:])
+        neg_half = keep.tile([P, BATCH], F32)
+        nc.vector.memset(neg_half[:], -0.5)
+
+        power = keep.tile([P, P], F32)
+        nc.vector.memset(power[:, 0:1], 1.0)
+        n = 1
+        while n < P:
+            nc.vector.tensor_scalar(
+                out=power[:, n : 2 * n], in0=power[:, 0:n], scalar1=DECAY ** (PACK * n), scalar2=None, op0=ALU.mult
+            )
+            n *= 2
+        freq = keep.tile([P, PACK, P], F32)
+        for t in range(PACK):
+            nc.vector.tensor_scalar(
+                out=freq[:, t, :], in0=power[:], scalar1=DECAY**t / (2.0 * math.pi), scalar2=None, op0=ALU.mult
+            )
+
+        w_perm = keep.tile([P, PASSES, PACK, P], BF16)
+        nc.vector.tensor_copy(out=w_perm[:], in_=w_raw[:].rearrange("f (g p t) -> f g t p", g=PASSES, t=PACK))
+        vec_f = keep.tile([P, 3, BLOCKS], F32)
+        nc.vector.tensor_copy(out=vec_f[:], in_=vec_bf[:, :, 0:BLOCKS])
+        bias_bc = keep.tile([P, N3], F32)
+        nc.vector.tensor_copy(out=bias_bc[:], in_=bias_bf[:])
+
+        xT = keep.tile([P, BATCH, GROUPS, P], BF16)
+        for b in range(BATCH):
+            xt_ps = psum_z.tile([P, GROUPS, P], BF16, tag="z")
+            for a in range(GROUPS):
+                nc.tensor.transpose(xt_ps[:, a, :], x_sb[:, b, a * FIN : (a + 1) * FIN], ident_bf[:])
+            nc.scalar.copy(out=xT[:, b, :, :], in_=xt_ps[:])
+
+        timing = {}
+        e_of = {}
+        sum_of = {}
+        sq_of = {}
+        scale_of = {}
+        shift_of = {}
+        n_of = {}
+        ht_of = {}
+        codes_of = {}
+        planes_of = {}
+
+        def timing_signal(a):
+            turns = phase.tile([P, PASSES, PACK * P], F32)
+            flat = freq[:].rearrange("p t c -> p (t c)")
+            nc.vector.tensor_scalar(
+                out=turns[:, 0, :], in0=flat, scalar1=pos[:, a : a + 1], scalar2=None, op0=ALU.mult
+            )
+            nc.vector.tensor_scalar(
+                out=turns[:, 1, :], in0=flat, scalar1=pos[:, a : a + 1], scalar2=0.25, op0=ALU.mult, op1=ALU.add
+            )
+            whole = phase.tile([P, PASSES, PACK * P], F32)
+            nc.vector.tensor_scalar(
+                out=whole[:], in0=turns[:], scalar1=ROUND_MAGIC, scalar2=ROUND_MAGIC, op0=ALU.add, op1=ALU.subtract
+            )
+            nc.vector.tensor_tensor(out=turns[:], in0=turns[:], in1=whole[:], op=ALU.subtract)
+            signal = phase.tile([P, PASSES, PACK * P], F32)
+            nc.scalar.activation(out=signal[:], in_=turns[:], func=ACT.Sin, scale=2.0 * math.pi)
+            timing[a] = signal
+
+        def embed(a, b):
+            if b == 0:
+                e_of[a] = rows.tile([P, BATCH, D], F32, name="e")
+                sum_of[a] = small.tile([P, BATCH, PASSES], F32, name="sum_e")
+                sq_of[a] = small.tile([P, BATCH], F32, name="sum_sq")
+            banks = []
+            for g in range(PASSES):
+                z = psum_z.tile([P, PACK * P], F32, tag="z")
+                nc.tensor.matmul(
+                    out=z[:],
+                    lhsT=xT[:, b, a, :],
+                    rhs=w_perm[:, g, :, :].rearrange("f t p -> f (t p)"),
+                    start=True,
+                    stop=False,
+                )
+                banks.append(z)
+            for g in range(PASSES):
+                for t in range(PACK):
+                    c = g * PACK + t
+                    nc.tensor.matmul(
+                        out=banks[g][:, t * P : (t + 1) * P],
+                        lhsT=vec_f[:, 0, c : c + 1].to_broadcast([P, P]),
+                        rhs=ident_f[:],
+                        is_transpose=True,
+                        start=False,
+                        stop=(t == PACK - 1),
+                    )
+            for g in range(PASSES):
+                nc.vector.scalar_tensor_tensor(
+                    out=e_of[a][:, b, g * 512 : (g + 1) * 512],
+                    in0=banks[g][:],
+                    scalar=0.0,
+                    in1=timing[a][:, g, :],
+                    op0=ALU.max,
+                    op1=ALU.add,
+                    accum_out=sum_of[a][:, b, g : g + 1],
+                )
+            squares = cols.tile([P, D], BF16)
+            nc.scalar.activation(
+                out=squares[:], in_=e_of[a][:, b, :], func=ACT.Square, accum_out=sq_of[a][:, b : b + 1]
+            )
+
+        def statistics(a):
+            mean = small.tile([P, BATCH], F32)
+            nc.vector.tensor_reduce(out=mean[:], in_=sum_of[a][:], axis=AX.X, op=ALU.add)
+            nc.vector.tensor_scalar(out=mean[:], in0=mean[:], scalar1=1.0 / D, scalar2=None, op0=ALU.mult)
+            mean_sq = small.tile([P, BATCH], F32)
+            nc.vector.tensor_tensor(out=mean_sq[:], in0=mean[:], in1=mean[:], op=ALU.mult)
+            var = small.tile([P, BATCH], F32)
+            nc.vector.tensor_scalar(
+                out=var[:], in0=sq_of[a][:], scalar1=1.0 / D, scalar2=EPS, op0=ALU.mult, op1=ALU.add
+            )
+            nc.vector.tensor_tensor(out=var[:], in0=var[:], in1=mean_sq[:], op=ALU.subtract)
+            rstd = small.tile([P, BATCH], F32)
+            nc.gpsimd.tensor_tensor(out=rstd[:], in0=var[:], in1=neg_half[:], op=ALU.pow)
+            shift = small.tile([P, BATCH], F32)
+            nc.vector.scalar_tensor_tensor(
+                out=shift[:], in0=mean[:], scalar=-1.0, in1=rstd[:], op0=ALU.mult, op1=ALU.mult
+            )
+            scale_of[a] = rstd
+            shift_of[a] = shift
+
+        def normalise(a, b):
+            if b == 0:
+                statistics(a)
+                n_of[a] = rows.tile([P, BATCH, D], F32, name="normed")
+            nc.scalar.activation(
+                out=n_of[a][:, b, :],
+                in_=e_of[a][:, b, :],
+                func=ACT.Identity,
+                scale=scale_of[a][:, b : b + 1],
+                bias=shift_of[a][:, b : b + 1],
+            )
+
+        def transpose_scale(a, quarter):
+            g = quarter // 2
+            if quarter % 2 == 0:
+                ht_of[a] = cols.tile([P, PACK, BATCH * P], BF16, name="ht")
+            if quarter == 0:
+                codes_of[a] = cols.tile([P, PASSES, BATCH * P], U32, name="codes", align_bytes=64)
+                planes_of[a] = cols.tile([P, PASSES, BATCH * P], U8, name="planes", align_bytes=64)
+            for t in (2 * (quarter % 2), 2 * (quarter % 2) + 1):
+                c = g * PACK + t
+                nt = psum_t.tile([P, BATCH, P], F32)
+                for b in range(BATCH):
+                    nc.tensor.transpose(nt[:, b, :], n_of[a][:, b, c * P : (c + 1) * P], ident_f[:])
+                nc.scalar.activation(
+                    out=ht_of[a][:, t, :],
+                    in_=nt[:].rearrange("p b k -> p (b k)"),
+                    func=ACT.Identity,
+                    scale=vec_f[:, 1, c : c + 1],
+                    bias=vec_f[:, 2, c : c + 1],
+                )
+            if quarter % 2 == 1:
+                grouped = cols.tile([P, BATCH * P, PACK], BF16, align_bytes=64)
+                nc.vector.tensor_copy(out=grouped[:], in_=ht_of[a][:].rearrange("p t k -> p k t"))
+                nc.vector.quantize_mx(
+                    out=codes_of[a][:, g, :].bitcast(FP8X4),
+                    scales=planes_of[a][:, g, :],
+                    in_=grouped[:].rearrange("p k t -> p (k t)"),
+                )
+
+        def project(a, b):
+            tok = slice(b * P, (b + 1) * P)
+            acc_qk = psum_o.tile([P, 2 * NOUT], F32)
+            acc_v = psum_o.tile([P, NOUT], F32)
+            for acc, n_cols in ((acc_qk, slice(0, 2 * NOUT)), (acc_v, slice(2 * NOUT, N3))):
+                for g in range(PASSES):
+                    nc.tensor.matmul_mx(
+                        out=acc[:],
+                        lhsT=codes_of[a][:, g, tok].bitcast(FP8X4),
+                        lhsT_scale=planes_of[a][:, g, tok],
+                        rhs=w_codes[:, g, n_cols].bitcast(FP8X4),
+                        rhs_scale=w_planes[:, g, n_cols],
+                        start=(g == 0),
+                        stop=(g == PASSES - 1),
+                    )
+            res = results.tile([P, N3], F32)
+            nc.vector.tensor_tensor(
+                out=res[:, 0 : 2 * NOUT], in0=acc_qk[:], in1=bias_bc[:, 0 : 2 * NOUT], op=ALU.add
+            )
+            nc.vector.tensor_tensor(out=res[:, 2 * NOUT : N3], in0=acc_v[:], in1=bias_bc[:, 2 * NOUT : N3], op=ALU.add)
+            for j, out in enumerate((out_0, out_1, out_2)):
+                nc.sync.dma_start(
+                    out=out[b].rearrange("(p a) n -> p a n", a=GROUPS)[:, a, :],
+                    in_=res[:, j * NOUT : (j + 1) * NOUT],
+                )
+
+        timing_signal(0)
+        for step in range(GROUPS + 3):
+            for quarter in range(BATCH):
+                if step >= 3:
+                    project(step - 3, quarter)
+                if 2 <= step < GROUPS + 2:
+                    transpose_scale(step - 2, quarter)
+                if 1 <= step < GROUPS + 1:
+                    normalise(step - 1, quarter)
+                if step < GROUPS:
+                    embed(step, quarter)
+                if quarter == 1 and step + 1 < GROUPS:
+                    timing_signal(step + 1)

@@ -12,7 +12,6 @@ U8 = mybir.dt.uint8
 FP8X4 = mybir.dt.float8_e4m3fn_x4
 ALU = mybir.AluOpType
 ACT = mybir.ActivationFunctionType
-AX = mybir.AxisListType
 
 P = 128
 BATCH = 4
@@ -149,19 +148,25 @@ def tile_ffnn_encoder_pa_t_kernel(
         def timing_signal(a):
             turns = phase.tile([P, PASSES, PACK * P], F32)
             flat = freq[:].rearrange("p t c -> p (t c)")
-            nc.vector.tensor_scalar(
-                out=turns[:, 0, :], in0=flat, scalar1=pos[:, a : a + 1], scalar2=None, op0=ALU.mult
-            )
-            nc.vector.tensor_scalar(
-                out=turns[:, 1, :], in0=flat, scalar1=pos[:, a : a + 1], scalar2=0.25, op0=ALU.mult, op1=ALU.add
-            )
+            for g in range(PASSES):
+                nc.gpsimd.tensor_scalar(
+                    out=turns[:, g, :],
+                    in0=flat,
+                    scalar1=pos[:, a : a + 1],
+                    scalar2=0.25 * g,
+                    op0=ALU.mult,
+                    op1=ALU.add,
+                )
             whole = phase.tile([P, PASSES, PACK * P], F32)
-            nc.vector.tensor_scalar(
-                out=whole[:], in0=turns[:], scalar1=ROUND_MAGIC, scalar2=ROUND_MAGIC, op0=ALU.add, op1=ALU.subtract
+            nc.gpsimd.tensor_scalar(
+                out=whole[:], in0=turns[:], scalar1=ROUND_MAGIC, scalar2=1.0, op0=ALU.add, op1=ALU.mult
             )
-            nc.vector.tensor_tensor(out=turns[:], in0=turns[:], in1=whole[:], op=ALU.subtract)
+            back = phase.tile([P, PASSES, PACK * P], F32)
+            nc.vector.scalar_tensor_tensor(
+                out=back[:], in0=whole[:], scalar=ROUND_MAGIC, in1=turns[:], op0=ALU.subtract, op1=ALU.subtract
+            )
             signal = phase.tile([P, PASSES, PACK * P], F32)
-            nc.scalar.activation(out=signal[:], in_=turns[:], func=ACT.Sin, scale=2.0 * math.pi)
+            nc.scalar.activation(out=signal[:], in_=back[:], func=ACT.Sin, scale=-2.0 * math.pi)
             timing[a] = signal
 
         def embed(a, b):
@@ -207,22 +212,22 @@ def tile_ffnn_encoder_pa_t_kernel(
             )
 
         def statistics(a):
-            mean = small.tile([P, BATCH], F32)
-            nc.vector.tensor_reduce(out=mean[:], in_=sum_of[a][:], axis=AX.X, op=ALU.add)
-            nc.vector.tensor_scalar(out=mean[:], in0=mean[:], scalar1=1.0 / D, scalar2=None, op0=ALU.mult)
+            neg_mean = small.tile([P, BATCH], F32)
+            nc.gpsimd.tensor_tensor(out=neg_mean[:], in0=sum_of[a][:, :, 0], in1=sum_of[a][:, :, 1], op=ALU.add)
+            nc.gpsimd.tensor_scalar(
+                out=neg_mean[:], in0=neg_mean[:], scalar1=-1.0 / D, scalar2=0.0, op0=ALU.mult, op1=ALU.add
+            )
             mean_sq = small.tile([P, BATCH], F32)
-            nc.vector.tensor_tensor(out=mean_sq[:], in0=mean[:], in1=mean[:], op=ALU.mult)
+            nc.gpsimd.tensor_tensor(out=mean_sq[:], in0=neg_mean[:], in1=neg_mean[:], op=ALU.mult)
             var = small.tile([P, BATCH], F32)
-            nc.vector.tensor_scalar(
+            nc.gpsimd.tensor_scalar(
                 out=var[:], in0=sq_of[a][:], scalar1=1.0 / D, scalar2=EPS, op0=ALU.mult, op1=ALU.add
             )
-            nc.vector.tensor_tensor(out=var[:], in0=var[:], in1=mean_sq[:], op=ALU.subtract)
+            nc.gpsimd.tensor_tensor(out=var[:], in0=var[:], in1=mean_sq[:], op=ALU.subtract)
             rstd = small.tile([P, BATCH], F32)
             nc.gpsimd.tensor_tensor(out=rstd[:], in0=var[:], in1=neg_half[:], op=ALU.pow)
             shift = small.tile([P, BATCH], F32)
-            nc.vector.scalar_tensor_tensor(
-                out=shift[:], in0=mean[:], scalar=-1.0, in1=rstd[:], op0=ALU.mult, op1=ALU.mult
-            )
+            nc.gpsimd.tensor_tensor(out=shift[:], in0=neg_mean[:], in1=rstd[:], op=ALU.mult)
             scale_of[a] = rstd
             shift_of[a] = shift
 
@@ -230,12 +235,13 @@ def tile_ffnn_encoder_pa_t_kernel(
             if b == 0:
                 statistics(a)
                 n_of[a] = rows.tile([P, BATCH, D], F32, name="normed")
-            nc.scalar.activation(
+            nc.gpsimd.tensor_scalar(
                 out=n_of[a][:, b, :],
-                in_=e_of[a][:, b, :],
-                func=ACT.Identity,
-                scale=scale_of[a][:, b : b + 1],
-                bias=shift_of[a][:, b : b + 1],
+                in0=e_of[a][:, b, :],
+                scalar1=scale_of[a][:, b : b + 1],
+                scalar2=shift_of[a][:, b : b + 1],
+                op0=ALU.mult,
+                op1=ALU.add,
             )
 
         def transpose_scale(a, quarter):
@@ -259,7 +265,12 @@ def tile_ffnn_encoder_pa_t_kernel(
                 )
             if quarter % 2 == 1:
                 grouped = cols.tile([P, BATCH * P, PACK], BF16, align_bytes=64)
-                nc.vector.tensor_copy(out=grouped[:], in_=ht_of[a][:].rearrange("p t k -> p k t"))
+                dst = grouped[:].rearrange("p (c i) t -> p c t i", i=4)
+                src = ht_of[a][:].rearrange("p t (c i) -> p c t i", i=4)
+                if g == 0:
+                    nc.vector.tensor_copy(out=dst, in_=src)
+                else:
+                    nc.scalar.copy(out=dst, in_=src)
                 nc.vector.quantize_mx(
                     out=codes_of[a][:, g, :].bitcast(FP8X4),
                     scales=planes_of[a][:, g, :],

@@ -22,11 +22,18 @@ NOUT = 256
 N3 = 3 * NOUT
 PACK = 4
 PASSES = D // (P * PACK)
+HALF = P * PACK
 BLOCKS = PASSES * PACK
 GROUPS = SEQ // P
+TILES = GROUPS * BATCH
 EPS = 1e-3
 ROUND_MAGIC = 12582912.0
 DECAY = math.exp(-math.log(10000.0) / 511.0)
+
+LAG_NORM = 5
+LAG_TRANSPOSE = 9
+LAG_PACK = 11
+LAG_PROJECT = 15
 
 FLOPS = 2 * BATCH * SEQ * FIN * D + 2 * BATCH * SEQ * D * N3
 
@@ -55,22 +62,23 @@ def tile_ffnn_encoder_pa_t_kernel(
     with ExitStack() as stack:
         keep = stack.enter_context(tc.tile_pool(name="keep", bufs=1))
         phase = stack.enter_context(tc.tile_pool(name="phase", bufs=2))
-        rows = stack.enter_context(tc.tile_pool(name="rows", bufs=2))
+        rows = stack.enter_context(tc.tile_pool(name="rows", bufs=3))
         small = stack.enter_context(tc.tile_pool(name="small", bufs=3))
         cols = stack.enter_context(tc.tile_pool(name="cols", bufs=2))
         results = stack.enter_context(tc.tile_pool(name="results", bufs=4))
         psum_z = stack.enter_context(tc.psum_pool(name="psum_z", bufs=4))
         psum_t = stack.enter_context(tc.psum_pool(name="psum_t", bufs=2))
         psum_o = stack.enter_context(tc.psum_pool(name="psum_o", bufs=1))
+        stack.enter_context(tc.manual_schedule())
 
+        w_raw = keep.tile([P, D], BF16)
+        nc.sync.dma_start(out=w_raw[:], in_=W_emb)
         x_sb = keep.tile([P, BATCH, GROUPS * FIN], BF16)
         for b in range(BATCH):
             nc.sync.dma_start(out=x_sb[:, b, :], in_=x[b].rearrange("(p a) f -> p (a f)", a=GROUPS))
-        w_raw = keep.tile([P, D], BF16)
-        nc.sync.dma_start(out=w_raw[:], in_=W_emb)
         vec_bf = keep.tile([P, 3, 16], BF16)
         for i, vec in enumerate((b_emb, g0, beta0)):
-            nc.sync.dma_start(
+            nc.scalar.dma_start(
                 out=vec_bf[:, i, 0:BLOCKS].rearrange("p (g t) -> p g t", t=PACK),
                 in_=vec.rearrange("(g p t) -> p g t", g=PASSES, t=PACK),
             )
@@ -79,32 +87,30 @@ def tile_ffnn_encoder_pa_t_kernel(
         nc.vector.memset(w_planes[:].rearrange("p g n -> p (g n)").bitcast(I32), 0)
         weights = ((Wq_words, Wq_scales, bq), (Wk_words, Wk_scales, bk), (Wv_words, Wv_scales, bv))
         for j, (words, scales, bias) in enumerate(weights):
-            n_cols = slice(j * NOUT, (j + 1) * NOUT)
             nc.sync.dma_start(
-                out=w_codes[:, :, n_cols].bitcast(I32),
+                out=w_codes[:, :, j * NOUT : (j + 1) * NOUT].bitcast(I32),
                 in_=words.rearrange("g p n t -> p g (n t)").bitcast(I32),
             )
         for j, (words, scales, bias) in enumerate(weights):
-            n_cols = slice(j * NOUT, (j + 1) * NOUT)
             for quad in range(4):
                 nc.sync.dma_start(
-                    out=w_planes[32 * quad : 32 * quad + 4, :, n_cols].bitcast(I32),
+                    out=w_planes[32 * quad : 32 * quad + 4, :, j * NOUT : (j + 1) * NOUT].bitcast(I32),
                     in_=scales.bitcast(I32)[:, 4 * quad : 4 * quad + 4, :].rearrange("g r n -> r g n"),
                 )
-        bias_bf = keep.tile([P, N3], BF16)
+        bias_bc = keep.tile([P, N3], BF16)
         for j, (words, scales, bias) in enumerate(weights):
-            nc.sync.dma_start(out=bias_bf[:, j * NOUT : (j + 1) * NOUT], in_=bias.partition_broadcast(P))
+            nc.sync.dma_start(out=bias_bc[:, j * NOUT : (j + 1) * NOUT], in_=bias.partition_broadcast(P))
 
+        pos_i = keep.tile([P, GROUPS], I32)
+        nc.gpsimd.iota(pos_i[:], pattern=[[1, GROUPS]], base=0, channel_multiplier=GROUPS)
         ident_bf = keep.tile([P, P], BF16)
         make_identity(nc, ident_bf[:])
         ident_f = keep.tile([P, P], F32)
         make_identity(nc, ident_f[:])
-        pos_i = keep.tile([P, GROUPS], I32)
-        nc.gpsimd.iota(pos_i[:], pattern=[[1, GROUPS]], base=0, channel_multiplier=GROUPS)
-        pos = keep.tile([P, GROUPS], F32)
-        nc.vector.tensor_copy(out=pos[:], in_=pos_i[:])
         neg_half = keep.tile([P, BATCH], F32)
         nc.vector.memset(neg_half[:], -0.5)
+        warm = keep.tile([P, 1], F32)
+        nc.scalar.activation(out=warm[:], in_=neg_half[:, 0:1], func=ACT.Sin)
 
         power = keep.tile([P, P], F32)
         nc.vector.memset(power[:, 0:1], 1.0)
@@ -119,13 +125,53 @@ def tile_ffnn_encoder_pa_t_kernel(
             nc.vector.tensor_scalar(
                 out=freq[:, t, :], in0=power[:], scalar1=DECAY**t / (2.0 * math.pi), scalar2=None, op0=ALU.mult
             )
+        pos = keep.tile([P, GROUPS], F32)
+        nc.vector.tensor_copy(out=pos[:], in_=pos_i[:])
+
+        turns_of = {}
+        timing = {}
+        z_of = {}
+        e_of = {}
+        sum_of = {}
+        sq_of = {}
+        scale_of = {}
+        shift_of = {}
+        n_of = {}
+        ht_of = {}
+        grouped_of = {}
+        codes_of = {}
+        planes_of = {}
+        acc_of = {}
+
+        def timing_turns(a):
+            turns = phase.tile([P, PASSES, HALF], F32)
+            flat = freq[:].rearrange("p t c -> p (t c)")
+            nc.vector.tensor_scalar(
+                out=turns[:, 0, :], in0=flat, scalar1=pos[:, a : a + 1], scalar2=None, op0=ALU.mult
+            )
+            nc.vector.tensor_scalar(
+                out=turns[:, 1, :], in0=flat, scalar1=pos[:, a : a + 1], scalar2=0.25, op0=ALU.mult, op1=ALU.add
+            )
+            whole = phase.tile([P, PASSES, HALF], F32)
+            nc.vector.tensor_scalar(
+                out=whole[:], in0=turns[:], scalar1=ROUND_MAGIC, scalar2=ROUND_MAGIC, op0=ALU.add, op1=ALU.subtract
+            )
+            turns_of[a] = (turns, whole)
+
+        def timing_signal(a):
+            turns, whole = turns_of[a]
+            nc.vector.tensor_tensor(out=turns[:], in0=turns[:], in1=whole[:], op=ALU.subtract)
+            signal = phase.tile([P, PASSES, HALF], F32)
+            nc.scalar.activation(out=signal[:], in_=turns[:], func=ACT.Sin, scale=2.0 * math.pi)
+            timing[a] = signal
+
+        timing_turns(0)
+        timing_signal(0)
 
         w_perm = keep.tile([P, PASSES, PACK, P], BF16)
         nc.vector.tensor_copy(out=w_perm[:], in_=w_raw[:].rearrange("f (g p t) -> f g t p", g=PASSES, t=PACK))
         vec_f = keep.tile([P, 3, BLOCKS], F32)
         nc.vector.tensor_copy(out=vec_f[:], in_=vec_bf[:, :, 0:BLOCKS])
-        bias_bc = keep.tile([P, N3], F32)
-        nc.vector.tensor_copy(out=bias_bc[:], in_=bias_bf[:])
 
         xT = keep.tile([P, BATCH, GROUPS, P], BF16)
         for b in range(BATCH):
@@ -134,49 +180,11 @@ def tile_ffnn_encoder_pa_t_kernel(
                 nc.tensor.transpose(xt_ps[:, a, :], x_sb[:, b, a * FIN : (a + 1) * FIN], ident_bf[:])
             nc.scalar.copy(out=xT[:, b, :, :], in_=xt_ps[:])
 
-        timing = {}
-        e_of = {}
-        sum_of = {}
-        sq_of = {}
-        scale_of = {}
-        shift_of = {}
-        n_of = {}
-        ht_of = {}
-        codes_of = {}
-        planes_of = {}
-
-        def timing_signal(a):
-            turns = phase.tile([P, PASSES, PACK * P], F32)
-            flat = freq[:].rearrange("p t c -> p (t c)")
-            for g in range(PASSES):
-                nc.gpsimd.tensor_scalar(
-                    out=turns[:, g, :],
-                    in0=flat,
-                    scalar1=pos[:, a : a + 1],
-                    scalar2=0.25 * g,
-                    op0=ALU.mult,
-                    op1=ALU.add,
-                )
-            whole = phase.tile([P, PASSES, PACK * P], F32)
-            nc.gpsimd.tensor_scalar(
-                out=whole[:], in0=turns[:], scalar1=ROUND_MAGIC, scalar2=1.0, op0=ALU.add, op1=ALU.mult
-            )
-            back = phase.tile([P, PASSES, PACK * P], F32)
-            nc.vector.scalar_tensor_tensor(
-                out=back[:], in0=whole[:], scalar=ROUND_MAGIC, in1=turns[:], op0=ALU.subtract, op1=ALU.subtract
-            )
-            signal = phase.tile([P, PASSES, PACK * P], F32)
-            nc.scalar.activation(out=signal[:], in_=back[:], func=ACT.Sin, scale=-2.0 * math.pi)
-            timing[a] = signal
-
-        def embed(a, b):
-            if b == 0:
-                e_of[a] = rows.tile([P, BATCH, D], F32, name="e")
-                sum_of[a] = small.tile([P, BATCH, PASSES], F32, name="sum_e")
-                sq_of[a] = small.tile([P, BATCH], F32, name="sum_sq")
+        def embed_matmuls(j):
+            a, b = divmod(j, BATCH)
             banks = []
             for g in range(PASSES):
-                z = psum_z.tile([P, PACK * P], F32, tag="z")
+                z = psum_z.tile([P, HALF], F32, tag="z")
                 nc.tensor.matmul(
                     out=z[:],
                     lhsT=xT[:, b, a, :],
@@ -196,16 +204,27 @@ def tile_ffnn_encoder_pa_t_kernel(
                         start=False,
                         stop=(t == PACK - 1),
                     )
+            z_of[j] = banks
+
+        def embed_rows(j):
+            a, b = divmod(j, BATCH)
+            if b == 0:
+                e_of[a] = rows.tile([P, BATCH, D], F32, name="e")
+                sum_of[a] = small.tile([P, BATCH, PASSES], F32, name="sum_e")
+                sq_of[a] = small.tile([P, BATCH], F32, name="sum_sq")
             for g in range(PASSES):
                 nc.vector.scalar_tensor_tensor(
-                    out=e_of[a][:, b, g * 512 : (g + 1) * 512],
-                    in0=banks[g][:],
+                    out=e_of[a][:, b, g * HALF : (g + 1) * HALF],
+                    in0=z_of[j][g][:],
                     scalar=0.0,
                     in1=timing[a][:, g, :],
                     op0=ALU.max,
                     op1=ALU.add,
                     accum_out=sum_of[a][:, b, g : g + 1],
                 )
+
+        def square_rows(j):
+            a, b = divmod(j, BATCH)
             squares = cols.tile([P, D], BF16)
             nc.scalar.activation(
                 out=squares[:], in_=e_of[a][:, b, :], func=ACT.Square, accum_out=sq_of[a][:, b : b + 1]
@@ -231,53 +250,58 @@ def tile_ffnn_encoder_pa_t_kernel(
             scale_of[a] = rstd
             shift_of[a] = shift
 
-        def normalise(a, b):
+        def normalise(j):
+            a, b = divmod(j, BATCH)
             if b == 0:
-                statistics(a)
                 n_of[a] = rows.tile([P, BATCH, D], F32, name="normed")
-            nc.gpsimd.tensor_scalar(
+            nc.scalar.activation(
                 out=n_of[a][:, b, :],
-                in0=e_of[a][:, b, :],
-                scalar1=scale_of[a][:, b : b + 1],
-                scalar2=shift_of[a][:, b : b + 1],
-                op0=ALU.mult,
-                op1=ALU.add,
+                in_=e_of[a][:, b, :],
+                func=ACT.Identity,
+                scale=scale_of[a][:, b : b + 1],
+                bias=shift_of[a][:, b : b + 1],
             )
 
-        def transpose_scale(a, quarter):
-            g = quarter // 2
-            if quarter % 2 == 0:
-                ht_of[a] = cols.tile([P, PACK, BATCH * P], BF16, name="ht")
-            if quarter == 0:
-                codes_of[a] = cols.tile([P, PASSES, BATCH * P], U32, name="codes", align_bytes=64)
-                planes_of[a] = cols.tile([P, PASSES, BATCH * P], U8, name="planes", align_bytes=64)
-            for t in (2 * (quarter % 2), 2 * (quarter % 2) + 1):
+        def transpose_scale(k):
+            a, quarter = divmod(k, BATCH)
+            g, pair = divmod(quarter, 2)
+            if pair == 0:
+                ht_of[a, g] = cols.tile([P, PACK, BATCH * P], BF16, name="ht")
+            for t in (2 * pair, 2 * pair + 1):
                 c = g * PACK + t
                 nt = psum_t.tile([P, BATCH, P], F32)
                 for b in range(BATCH):
                     nc.tensor.transpose(nt[:, b, :], n_of[a][:, b, c * P : (c + 1) * P], ident_f[:])
                 nc.scalar.activation(
-                    out=ht_of[a][:, t, :],
+                    out=ht_of[a, g][:, t, :],
                     in_=nt[:].rearrange("p b k -> p (b k)"),
                     func=ACT.Identity,
                     scale=vec_f[:, 1, c : c + 1],
                     bias=vec_f[:, 2, c : c + 1],
                 )
-            if quarter % 2 == 1:
+
+        def pack(m):
+            a, piece = divmod(m, BATCH)
+            g, quantise = divmod(piece, 2)
+            if piece == 0:
+                codes_of[a] = cols.tile([P, PASSES, BATCH * P], U32, name="codes", align_bytes=64)
+                planes_of[a] = cols.tile([P, PASSES, BATCH * P], U8, name="planes", align_bytes=64)
+            if not quantise:
                 grouped = cols.tile([P, BATCH * P, PACK], BF16, align_bytes=64)
-                dst = grouped[:].rearrange("p (c i) t -> p c t i", i=4)
-                src = ht_of[a][:].rearrange("p t (c i) -> p c t i", i=4)
-                if g == 0:
-                    nc.vector.tensor_copy(out=dst, in_=src)
-                else:
-                    nc.scalar.copy(out=dst, in_=src)
+                nc.vector.tensor_copy(
+                    out=grouped[:].rearrange("p (c i) t -> p c t i", i=4),
+                    in_=ht_of[a, g][:].rearrange("p t (c i) -> p c t i", i=4),
+                )
+                grouped_of[a, g] = grouped
+            else:
                 nc.vector.quantize_mx(
                     out=codes_of[a][:, g, :].bitcast(FP8X4),
                     scales=planes_of[a][:, g, :],
-                    in_=grouped[:].rearrange("p k t -> p (k t)"),
+                    in_=grouped_of[a, g][:].rearrange("p k t -> p (k t)"),
                 )
 
-        def project(a, b):
+        def project_matmuls(j):
+            a, b = divmod(j, BATCH)
             tok = slice(b * P, (b + 1) * P)
             acc_qk = psum_o.tile([P, 2 * NOUT], F32)
             acc_v = psum_o.tile([P, NOUT], F32)
@@ -292,27 +316,46 @@ def tile_ffnn_encoder_pa_t_kernel(
                         start=(g == 0),
                         stop=(g == PASSES - 1),
                     )
+            acc_of[j] = (acc_qk, acc_v)
+
+        def project_store(j):
+            a, b = divmod(j, BATCH)
+            acc_qk, acc_v = acc_of[j]
             res = results.tile([P, N3], F32)
             nc.vector.tensor_tensor(
                 out=res[:, 0 : 2 * NOUT], in0=acc_qk[:], in1=bias_bc[:, 0 : 2 * NOUT], op=ALU.add
             )
             nc.vector.tensor_tensor(out=res[:, 2 * NOUT : N3], in0=acc_v[:], in1=bias_bc[:, 2 * NOUT : N3], op=ALU.add)
-            for j, out in enumerate((out_0, out_1, out_2)):
+            for i, out in enumerate((out_0, out_1, out_2)):
                 nc.sync.dma_start(
                     out=out[b].rearrange("(p a) n -> p a n", a=GROUPS)[:, a, :],
-                    in_=res[:, j * NOUT : (j + 1) * NOUT],
+                    in_=res[:, i * NOUT : (i + 1) * NOUT],
                 )
 
-        timing_signal(0)
-        for step in range(GROUPS + 3):
-            for quarter in range(BATCH):
-                if step >= 3:
-                    project(step - 3, quarter)
-                if 2 <= step < GROUPS + 2:
-                    transpose_scale(step - 2, quarter)
-                if 1 <= step < GROUPS + 1:
-                    normalise(step - 1, quarter)
-                if step < GROUPS:
-                    embed(step, quarter)
-                if quarter == 1 and step + 1 < GROUPS:
-                    timing_signal(step + 1)
+        def in_range(j):
+            return 0 <= j < TILES
+
+        embed_matmuls(0)
+        for turn in range(TILES + LAG_PROJECT):
+            if in_range(turn - LAG_PROJECT):
+                project_matmuls(turn - LAG_PROJECT)
+            if in_range(turn):
+                embed_rows(turn)
+            if in_range(turn - 1):
+                square_rows(turn - 1)
+            if turn % BATCH == 0 and in_range(turn - BATCH):
+                statistics(turn // BATCH - 1)
+            if in_range(turn - LAG_TRANSPOSE):
+                transpose_scale(turn - LAG_TRANSPOSE)
+            if in_range(turn - LAG_PROJECT):
+                project_store(turn - LAG_PROJECT)
+            if in_range(turn - LAG_NORM):
+                normalise(turn - LAG_NORM)
+            if in_range(turn + 1):
+                embed_matmuls(turn + 1)
+            if in_range(turn - LAG_PACK):
+                pack(turn - LAG_PACK)
+            if turn % BATCH == 0 and in_range(turn + BATCH):
+                timing_turns(turn // BATCH + 1)
+            if turn % BATCH == 2 and in_range(turn + 2):
+                timing_signal(turn // BATCH + 1)

@@ -29,6 +29,8 @@ TILES = GROUPS * BATCH
 EPS = 1e-3
 ROUND_MAGIC = 12582912.0
 DECAY = math.exp(-math.log(10000.0) / 511.0)
+FIRST_SMALL = math.ceil(511.0 * math.log(2.0 * (SEQ - 1) / math.pi) / math.log(10000.0))
+WRAP = -(-FIRST_SMALL // PACK)
 
 LAG_NORM = 5
 LAG_TRANSPOSE = 9
@@ -66,9 +68,8 @@ def tile_ffnn_encoder_pa_t_kernel(
         small = stack.enter_context(tc.tile_pool(name="small", bufs=3))
         cols = stack.enter_context(tc.tile_pool(name="cols", bufs=2))
         results = stack.enter_context(tc.tile_pool(name="results", bufs=4))
-        psum_z = stack.enter_context(tc.psum_pool(name="psum_z", bufs=4))
+        psum_z = stack.enter_context(tc.psum_pool(name="psum_z", bufs=6))
         psum_t = stack.enter_context(tc.psum_pool(name="psum_t", bufs=2))
-        psum_o = stack.enter_context(tc.psum_pool(name="psum_o", bufs=1))
         stack.enter_context(tc.manual_schedule())
 
         w_raw = keep.tile([P, D], BF16)
@@ -152,15 +153,21 @@ def tile_ffnn_encoder_pa_t_kernel(
             nc.vector.tensor_scalar(
                 out=turns[:, 1, :], in0=flat, scalar1=pos[:, a : a + 1], scalar2=0.25, op0=ALU.mult, op1=ALU.add
             )
-            whole = phase.tile([P, PASSES, HALF], F32)
+            whole = phase.tile([P, BLOCKS, WRAP], F32)
             nc.vector.tensor_scalar(
-                out=whole[:], in0=turns[:], scalar1=ROUND_MAGIC, scalar2=ROUND_MAGIC, op0=ALU.add, op1=ALU.subtract
+                out=whole[:],
+                in0=turns[:].rearrange("p g (t c) -> p (g t) c", c=P)[:, :, 0:WRAP],
+                scalar1=ROUND_MAGIC,
+                scalar2=ROUND_MAGIC,
+                op0=ALU.add,
+                op1=ALU.subtract,
             )
             turns_of[a] = (turns, whole)
 
         def timing_signal(a):
             turns, whole = turns_of[a]
-            nc.vector.tensor_tensor(out=turns[:], in0=turns[:], in1=whole[:], op=ALU.subtract)
+            wrapped = turns[:].rearrange("p g (t c) -> p (g t) c", c=P)[:, :, 0:WRAP]
+            nc.vector.tensor_tensor(out=wrapped, in0=wrapped, in1=whole[:], op=ALU.subtract)
             signal = phase.tile([P, PASSES, HALF], F32)
             nc.scalar.activation(out=signal[:], in_=turns[:], func=ACT.Sin, scale=2.0 * math.pi)
             timing[a] = signal
@@ -254,13 +261,23 @@ def tile_ffnn_encoder_pa_t_kernel(
             a, b = divmod(j, BATCH)
             if b == 0:
                 n_of[a] = rows.tile([P, BATCH, D], F32, name="normed")
-            nc.scalar.activation(
-                out=n_of[a][:, b, :],
-                in_=e_of[a][:, b, :],
-                func=ACT.Identity,
-                scale=scale_of[a][:, b : b + 1],
-                bias=shift_of[a][:, b : b + 1],
-            )
+            if b == 1:
+                nc.vector.tensor_scalar(
+                    out=n_of[a][:, b, :],
+                    in0=e_of[a][:, b, :],
+                    scalar1=scale_of[a][:, b : b + 1],
+                    scalar2=shift_of[a][:, b : b + 1],
+                    op0=ALU.mult,
+                    op1=ALU.add,
+                )
+            else:
+                nc.scalar.activation(
+                    out=n_of[a][:, b, :],
+                    in_=e_of[a][:, b, :],
+                    func=ACT.Identity,
+                    scale=scale_of[a][:, b : b + 1],
+                    bias=shift_of[a][:, b : b + 1],
+                )
 
         def transpose_scale(k):
             a, quarter = divmod(k, BATCH)
@@ -303,8 +320,8 @@ def tile_ffnn_encoder_pa_t_kernel(
         def project_matmuls(j):
             a, b = divmod(j, BATCH)
             tok = slice(b * P, (b + 1) * P)
-            acc_qk = psum_o.tile([P, 2 * NOUT], F32)
-            acc_v = psum_o.tile([P, NOUT], F32)
+            acc_qk = psum_z.tile([P, 2 * NOUT], F32, tag="z")
+            acc_v = psum_z.tile([P, NOUT], F32, tag="z")
             for acc, n_cols in ((acc_qk, slice(0, 2 * NOUT)), (acc_v, slice(2 * NOUT, N3))):
                 for g in range(PASSES):
                     nc.tensor.matmul_mx(

@@ -147,41 +147,53 @@ def tile_ffnn_encoder_pa_t_kernel(
         def timing_turns(a):
             turns = phase.tile([P, PASSES, HALF], F32)
             flat = freq[:].rearrange("p t c -> p (t c)")
-            nc.vector.tensor_scalar(
-                out=turns[:, 0, :], in0=flat, scalar1=pos[:, a : a + 1], scalar2=None, op0=ALU.mult
-            )
-            nc.vector.tensor_scalar(
-                out=turns[:, 1, :], in0=flat, scalar1=pos[:, a : a + 1], scalar2=0.25, op0=ALU.mult, op1=ALU.add
-            )
+            for g in range(PASSES):
+                nc.gpsimd.tensor_scalar(
+                    out=turns[:, g, :],
+                    in0=flat,
+                    scalar1=pos[:, a : a + 1],
+                    scalar2=0.25 * g,
+                    op0=ALU.mult,
+                    op1=ALU.add,
+                )
             whole = phase.tile([P, BLOCKS, WRAP], F32)
-            nc.vector.tensor_scalar(
+            nc.gpsimd.tensor_scalar(
                 out=whole[:],
                 in0=turns[:].rearrange("p g (t c) -> p (g t) c", c=P)[:, :, 0:WRAP],
-                scalar1=ROUND_MAGIC,
+                scalar1=-1.0,
                 scalar2=ROUND_MAGIC,
-                op0=ALU.add,
-                op1=ALU.subtract,
+                op0=ALU.mult,
+                op1=ALU.add,
             )
             turns_of[a] = (turns, whole)
 
-        def timing_signal(a):
+        def timing_wrap(a):
             turns, whole = turns_of[a]
             wrapped = turns[:].rearrange("p g (t c) -> p (g t) c", c=P)[:, :, 0:WRAP]
-            nc.vector.tensor_tensor(out=wrapped, in0=wrapped, in1=whole[:], op=ALU.subtract)
+            nc.vector.scalar_tensor_tensor(
+                out=wrapped, in0=whole[:], scalar=ROUND_MAGIC, in1=wrapped, op0=ALU.subtract, op1=ALU.add
+            )
+
+        def timing_signal(a):
+            turns, whole = turns_of[a]
             signal = phase.tile([P, PASSES, HALF], F32)
             nc.scalar.activation(out=signal[:], in_=turns[:], func=ACT.Sin, scale=2.0 * math.pi)
             timing[a] = signal
 
         timing_turns(0)
-        timing_signal(0)
+        timing_turns(1)
 
         w_perm = keep.tile([P, PASSES, PACK, P], BF16)
         nc.vector.tensor_copy(out=w_perm[:], in_=w_raw[:].rearrange("f (g p t) -> f g t p", g=PASSES, t=PACK))
         vec_f = keep.tile([P, 3, BLOCKS], F32)
         nc.vector.tensor_copy(out=vec_f[:], in_=vec_bf[:, :, 0:BLOCKS])
 
+        timing_wrap(0)
+        timing_wrap(1)
+
         xT = keep.tile([P, BATCH, GROUPS, P], BF16)
-        for b in range(BATCH):
+
+        def transpose_x(b):
             xt_ps = psum_z.tile([P, GROUPS, P], BF16, tag="z")
             for a in range(GROUPS):
                 nc.tensor.transpose(xt_ps[:, a, :], x_sb[:, b, a * FIN : (a + 1) * FIN], ident_bf[:])
@@ -189,6 +201,8 @@ def tile_ffnn_encoder_pa_t_kernel(
 
         def embed_matmuls(j):
             a, b = divmod(j, BATCH)
+            if a == 0:
+                transpose_x(b)
             banks = []
             for g in range(PASSES):
                 z = psum_z.tile([P, HALF], F32, tag="z")
@@ -261,7 +275,7 @@ def tile_ffnn_encoder_pa_t_kernel(
             a, b = divmod(j, BATCH)
             if b == 0:
                 n_of[a] = rows.tile([P, BATCH, D], F32, name="normed")
-            if b == 1:
+            if b == BATCH - 1:
                 nc.vector.tensor_scalar(
                     out=n_of[a][:, b, :],
                     in0=e_of[a][:, b, :],
@@ -353,6 +367,7 @@ def tile_ffnn_encoder_pa_t_kernel(
             return 0 <= j < TILES
 
         embed_matmuls(0)
+        timing_signal(0)
         for turn in range(TILES + LAG_PROJECT):
             if in_range(turn - LAG_PROJECT):
                 project_matmuls(turn - LAG_PROJECT)
@@ -373,6 +388,8 @@ def tile_ffnn_encoder_pa_t_kernel(
             if in_range(turn - LAG_PACK):
                 pack(turn - LAG_PACK)
             if turn % BATCH == 0 and in_range(turn + BATCH):
-                timing_turns(turn // BATCH + 1)
-            if turn % BATCH == 2 and in_range(turn + 2):
                 timing_signal(turn // BATCH + 1)
+            if turn % BATCH == 0 and in_range(turn + 2 * BATCH):
+                timing_turns(turn // BATCH + 2)
+            if turn % BATCH == 2 and in_range(turn + 6):
+                timing_wrap(turn // BATCH + 2)

@@ -34,8 +34,9 @@ WRAP = -(-FIRST_SMALL // PACK)
 
 LAG_NORM = 5
 LAG_TRANSPOSE = 9
-LAG_PACK = 11
-LAG_PROJECT = 15
+LAG_SCALE = 10
+LAG_PACK = 12
+LAG_PROJECT = 16
 
 FLOPS = 2 * BATCH * SEQ * FIN * D + 2 * BATCH * SEQ * D * N3
 
@@ -138,6 +139,7 @@ def tile_ffnn_encoder_pa_t_kernel(
         scale_of = {}
         shift_of = {}
         n_of = {}
+        nt_of = {}
         ht_of = {}
         grouped_of = {}
         codes_of = {}
@@ -199,33 +201,35 @@ def tile_ffnn_encoder_pa_t_kernel(
                 nc.tensor.transpose(xt_ps[:, a, :], x_sb[:, b, a * FIN : (a + 1) * FIN], ident_bf[:])
             nc.scalar.copy(out=xT[:, b, :, :], in_=xt_ps[:])
 
-        def embed_matmuls(j):
+        def embed_bias(j):
             a, b = divmod(j, BATCH)
             if a == 0:
                 transpose_x(b)
             banks = []
             for g in range(PASSES):
                 z = psum_z.tile([P, HALF], F32, tag="z")
-                nc.tensor.matmul(
-                    out=z[:],
-                    lhsT=xT[:, b, a, :],
-                    rhs=w_perm[:, g, :, :].rearrange("f t p -> f (t p)"),
-                    start=True,
-                    stop=False,
-                )
-                banks.append(z)
-            for g in range(PASSES):
                 for t in range(PACK):
                     c = g * PACK + t
                     nc.tensor.matmul(
-                        out=banks[g][:, t * P : (t + 1) * P],
+                        out=z[:, t * P : (t + 1) * P],
                         lhsT=vec_f[:, 0, c : c + 1].to_broadcast([P, P]),
                         rhs=ident_f[:],
                         is_transpose=True,
-                        start=False,
-                        stop=(t == PACK - 1),
+                        start=(t == 0),
+                        stop=False,
                     )
+                banks.append(z)
             z_of[j] = banks
+
+        def embed_matmul(j, g):
+            a, b = divmod(j, BATCH)
+            nc.tensor.matmul(
+                out=z_of[j][g][:],
+                lhsT=xT[:, b, a, :],
+                rhs=w_perm[:, g, :, :].rearrange("f t p -> f (t p)"),
+                start=False,
+                stop=True,
+            )
 
         def embed_rows(j):
             a, b = divmod(j, BATCH)
@@ -275,7 +279,7 @@ def tile_ffnn_encoder_pa_t_kernel(
             a, b = divmod(j, BATCH)
             if b == 0:
                 n_of[a] = rows.tile([P, BATCH, D], F32, name="normed")
-            if b == BATCH - 1:
+            if b == 0:
                 nc.vector.tensor_scalar(
                     out=n_of[a][:, b, :],
                     in0=e_of[a][:, b, :],
@@ -293,19 +297,23 @@ def tile_ffnn_encoder_pa_t_kernel(
                     bias=shift_of[a][:, b : b + 1],
                 )
 
-        def transpose_scale(k):
+        def transpose_blocks(k):
             a, quarter = divmod(k, BATCH)
-            g, pair = divmod(quarter, 2)
-            if pair == 0:
-                ht_of[a, g] = cols.tile([P, PACK, BATCH * P], BF16, name="ht")
-            for t in (2 * pair, 2 * pair + 1):
-                c = g * PACK + t
+            for c in (2 * quarter, 2 * quarter + 1):
                 nt = psum_t.tile([P, BATCH, P], F32)
                 for b in range(BATCH):
                     nc.tensor.transpose(nt[:, b, :], n_of[a][:, b, c * P : (c + 1) * P], ident_f[:])
+                nt_of[a, c] = nt
+
+        def scale_blocks(k):
+            a, quarter = divmod(k, BATCH)
+            for c in (2 * quarter, 2 * quarter + 1):
+                g, t = divmod(c, PACK)
+                if t == 0:
+                    ht_of[a, g] = cols.tile([P, PACK, BATCH * P], BF16, name="ht")
                 nc.scalar.activation(
                     out=ht_of[a, g][:, t, :],
-                    in_=nt[:].rearrange("p b k -> p (b k)"),
+                    in_=nt_of[a, c][:].rearrange("p b k -> p (b k)"),
                     func=ACT.Identity,
                     scale=vec_f[:, 1, c : c + 1],
                     bias=vec_f[:, 2, c : c + 1],
@@ -366,30 +374,37 @@ def tile_ffnn_encoder_pa_t_kernel(
         def in_range(j):
             return 0 <= j < TILES
 
-        embed_matmuls(0)
+        embed_bias(0)
+        embed_matmul(0, 0)
+        embed_matmul(0, 1)
         timing_signal(0)
         for turn in range(TILES + LAG_PROJECT):
+            if in_range(turn + 1):
+                embed_bias(turn + 1)
+                embed_matmul(turn + 1, 0)
             if in_range(turn - LAG_PROJECT):
                 project_matmuls(turn - LAG_PROJECT)
+            if in_range(turn + 1):
+                embed_matmul(turn + 1, 1)
             if in_range(turn):
                 embed_rows(turn)
             if in_range(turn - 1):
                 square_rows(turn - 1)
             if turn % BATCH == 0 and in_range(turn - BATCH):
                 statistics(turn // BATCH - 1)
+            if in_range(turn - LAG_SCALE):
+                scale_blocks(turn - LAG_SCALE)
             if in_range(turn - LAG_TRANSPOSE):
-                transpose_scale(turn - LAG_TRANSPOSE)
+                transpose_blocks(turn - LAG_TRANSPOSE)
             if in_range(turn - LAG_PROJECT):
                 project_store(turn - LAG_PROJECT)
             if in_range(turn - LAG_NORM):
                 normalise(turn - LAG_NORM)
-            if in_range(turn + 1):
-                embed_matmuls(turn + 1)
             if in_range(turn - LAG_PACK):
                 pack(turn - LAG_PACK)
-            if turn % BATCH == 0 and in_range(turn + BATCH):
-                timing_signal(turn // BATCH + 1)
-            if turn % BATCH == 0 and in_range(turn + 2 * BATCH):
-                timing_turns(turn // BATCH + 2)
-            if turn % BATCH == 2 and in_range(turn + 6):
-                timing_wrap(turn // BATCH + 2)
+            if turn % BATCH == 1 and in_range(turn + 3):
+                timing_signal((turn + 3) // BATCH)
+            if turn % BATCH == 1 and in_range(turn + 7):
+                timing_turns((turn + 7) // BATCH)
+            if turn % BATCH == 3 and in_range(turn + 5):
+                timing_wrap((turn + 5) // BATCH)

@@ -279,7 +279,7 @@ def tile_ffnn_encoder_pa_t_kernel(
             a, b = divmod(j, BATCH)
             if b == 0:
                 n_of[a] = rows.tile([P, BATCH, D], F32, name="normed")
-            if b == 0:
+            if b == 0 or j + LAG_NORM < LAG_PROJECT:
                 nc.vector.tensor_scalar(
                     out=n_of[a][:, b, :],
                     in0=e_of[a][:, b, :],

@@ -131,6 +131,7 @@ def tile_ffnn_encoder_pa_t_kernel(
         nc.vector.tensor_copy(out=pos[:], in_=pos_i[:])
 
         turns_of = {}
+        mean_of = {}
         timing = {}
         z_of = {}
         e_of = {}
@@ -252,22 +253,28 @@ def tile_ffnn_encoder_pa_t_kernel(
             a, b = divmod(j, BATCH)
             squares = cols.tile([P, D], BF16)
             nc.scalar.activation(
-                out=squares[:], in_=e_of[a][:, b, :], func=ACT.Square, accum_out=sq_of[a][:, b : b + 1]
+                out=squares[:],
+                in_=e_of[a][:, b, :],
+                func=ACT.Square,
+                scale=1.0 / math.sqrt(D),
+                accum_out=sq_of[a][:, b : b + 1],
             )
 
-        def statistics(a):
+        def mean_part(a):
             neg_mean = small.tile([P, BATCH], F32)
             nc.gpsimd.tensor_tensor(out=neg_mean[:], in0=sum_of[a][:, :, 0], in1=sum_of[a][:, :, 1], op=ALU.add)
             nc.gpsimd.tensor_scalar(
                 out=neg_mean[:], in0=neg_mean[:], scalar1=-1.0 / D, scalar2=0.0, op0=ALU.mult, op1=ALU.add
             )
-            mean_sq = small.tile([P, BATCH], F32)
-            nc.gpsimd.tensor_tensor(out=mean_sq[:], in0=neg_mean[:], in1=neg_mean[:], op=ALU.mult)
+            rest = small.tile([P, BATCH], F32)
+            nc.gpsimd.tensor_tensor(out=rest[:], in0=neg_mean[:], in1=neg_mean[:], op=ALU.mult)
+            nc.gpsimd.tensor_scalar(out=rest[:], in0=rest[:], scalar1=-1.0, scalar2=EPS, op0=ALU.mult, op1=ALU.add)
+            mean_of[a] = (neg_mean, rest)
+
+        def statistics(a):
+            neg_mean, rest = mean_of[a]
             var = small.tile([P, BATCH], F32)
-            nc.gpsimd.tensor_scalar(
-                out=var[:], in0=sq_of[a][:], scalar1=1.0 / D, scalar2=EPS, op0=ALU.mult, op1=ALU.add
-            )
-            nc.gpsimd.tensor_tensor(out=var[:], in0=var[:], in1=mean_sq[:], op=ALU.subtract)
+            nc.gpsimd.tensor_tensor(out=var[:], in0=sq_of[a][:], in1=rest[:], op=ALU.add)
             rstd = small.tile([P, BATCH], F32)
             nc.gpsimd.tensor_tensor(out=rstd[:], in0=var[:], in1=neg_half[:], op=ALU.pow)
             shift = small.tile([P, BATCH], F32)
@@ -388,6 +395,8 @@ def tile_ffnn_encoder_pa_t_kernel(
                 embed_matmul(turn + 1, 1)
             if in_range(turn):
                 embed_rows(turn)
+                if turn % BATCH == BATCH - 1:
+                    mean_part(turn // BATCH)
             if in_range(turn - 1):
                 square_rows(turn - 1)
             if turn % BATCH == 0 and in_range(turn - BATCH):

@@ -37,6 +37,7 @@ LAG_TRANSPOSE = 9
 LAG_SCALE = 10
 LAG_PACK = 12
 LAG_PROJECT = 16
+LAG_STORE = 17
 
 FLOPS = 2 * BATCH * SEQ * FIN * D + 2 * BATCH * SEQ * D * N3
 
@@ -385,7 +386,7 @@ def tile_ffnn_encoder_pa_t_kernel(
         embed_matmul(0, 0)
         embed_matmul(0, 1)
         timing_signal(0)
-        for turn in range(TILES + LAG_PROJECT):
+        for turn in range(TILES + LAG_STORE):
             if in_range(turn + 1):
                 embed_bias(turn + 1)
                 embed_matmul(turn + 1, 0)
@@ -405,8 +406,8 @@ def tile_ffnn_encoder_pa_t_kernel(
                 scale_blocks(turn - LAG_SCALE)
             if in_range(turn - LAG_TRANSPOSE):
                 transpose_blocks(turn - LAG_TRANSPOSE)
-            if in_range(turn - LAG_PROJECT):
-                project_store(turn - LAG_PROJECT)
+            if in_range(turn - LAG_STORE):
+                project_store(turn - LAG_STORE)
             if in_range(turn - LAG_NORM):
                 normalise(turn - LAG_NORM)
             if in_range(turn - LAG_PACK):

@@ -287,7 +287,7 @@ def tile_ffnn_encoder_pa_t_kernel(
             a, b = divmod(j, BATCH)
             if b == 0:
                 n_of[a] = rows.tile([P, BATCH, D], F32, name="normed")
-            if b == 0 or j + LAG_NORM < LAG_PROJECT:
+            if b == 0 or (b == 2 and j + LAG_NORM < LAG_PROJECT):
                 nc.vector.tensor_scalar(
                     out=n_of[a][:, b, :],
                     in0=e_of[a][:, b, :],

@@ -74,11 +74,12 @@ def tile_ffnn_encoder_pa_t_kernel(
         psum_t = stack.enter_context(tc.psum_pool(name="psum_t", bufs=2))
         stack.enter_context(tc.manual_schedule())
 
-        w_raw = keep.tile([P, D], BF16)
-        nc.sync.dma_start(out=w_raw[:], in_=W_emb)
         x_sb = keep.tile([P, BATCH, GROUPS * FIN], BF16)
+        w_raw = keep.tile([P, D], BF16)
         for b in range(BATCH):
             nc.sync.dma_start(out=x_sb[:, b, :], in_=x[b].rearrange("(p a) f -> p (a f)", a=GROUPS))
+            if b == 0:
+                nc.sync.dma_start(out=w_raw[:], in_=W_emb)
         vec_bf = keep.tile([P, 3, 16], BF16)
         for i, vec in enumerate((b_emb, g0, beta0)):
             nc.scalar.dma_start(
@@ -287,7 +288,7 @@ def tile_ffnn_encoder_pa_t_kernel(
             a, b = divmod(j, BATCH)
             if b == 0:
                 n_of[a] = rows.tile([P, BATCH, D], F32, name="normed")
-            if b == 0 or (b == 2 and j + LAG_NORM < LAG_PROJECT):
+            if b == 0 or (b == 2 and j + LAG_NORM < LAG_PROJECT) or LAG_SCALE <= j + LAG_NORM < LAG_PACK:
                 nc.vector.tensor_scalar(
                     out=n_of[a][:, b, :],
                     in0=e_of[a][:, b, :],
@@ -335,10 +336,16 @@ def tile_ffnn_encoder_pa_t_kernel(
                 planes_of[a] = cols.tile([P, PASSES, BATCH * P], U8, name="planes", align_bytes=64)
             if not quantise:
                 grouped = cols.tile([P, BATCH * P, PACK], BF16, align_bytes=64)
+                mine = (BATCH - 1) * P if m + LAG_PACK >= TILES + LAG_NORM else BATCH * P
                 nc.vector.tensor_copy(
-                    out=grouped[:].rearrange("p (c i) t -> p c t i", i=4),
-                    in_=ht_of[a, g][:].rearrange("p t (c i) -> p c t i", i=4),
+                    out=grouped[:, 0:mine, :].rearrange("p (c i) t -> p c t i", i=4),
+                    in_=ht_of[a, g][:, :, 0:mine].rearrange("p t (c i) -> p c t i", i=4),
                 )
+                if mine < BATCH * P:
+                    nc.scalar.copy(
+                        out=grouped[:, mine : BATCH * P, :].rearrange("p (c i) t -> p c t i", i=4),
+                        in_=ht_of[a, g][:, :, mine : BATCH * P].rearrange("p t (c i) -> p c t i", i=4),
+                    )
                 grouped_of[a, g] = grouped
             else:
                 nc.vector.quantize_mx(

@@ -27,7 +27,6 @@ BLOCKS = PASSES * PACK
 GROUPS = SEQ // P
 TILES = GROUPS * BATCH
 EPS = 1e-3
-ROUND_MAGIC = 12582912.0
 DECAY = math.exp(-math.log(10000.0) / 511.0)
 FIRST_SMALL = math.ceil(511.0 * math.log(2.0 * (SEQ - 1) / math.pi) / math.log(10000.0))
 WRAP = -(-FIRST_SMALL // PACK)
@@ -131,8 +130,12 @@ def tile_ffnn_encoder_pa_t_kernel(
             )
         pos = keep.tile([P, GROUPS], F32)
         nc.vector.tensor_copy(out=pos[:], in_=pos_i[:])
+        pos_rad = keep.tile([P, GROUPS], F32)
+        nc.vector.tensor_scalar(out=pos_rad[:], in0=pos[:], scalar1=2.0 * math.pi, scalar2=None, op0=ALU.mult)
 
-        turns_of = {}
+        whole_of = {}
+        reduced_of = {}
+        folded_of = {}
         mean_of = {}
         timing = {}
         z_of = {}
@@ -149,52 +152,67 @@ def tile_ffnn_encoder_pa_t_kernel(
         planes_of = {}
         acc_of = {}
 
-        def timing_turns(a):
-            turns = phase.tile([P, PASSES, HALF], F32)
-            flat = freq[:].rearrange("p t c -> p (t c)")
-            for g in range(PASSES):
-                nc.gpsimd.tensor_scalar(
-                    out=turns[:, g, :],
-                    in0=flat,
-                    scalar1=pos[:, a : a + 1],
-                    scalar2=0.25 * g,
-                    op0=ALU.mult,
-                    op1=ALU.add,
-                )
-            whole = phase.tile([P, BLOCKS, WRAP], F32)
+        def timing_whole(a):
+            whole = phase.tile([P, PACK, WRAP], I32)
             nc.gpsimd.tensor_scalar(
                 out=whole[:],
-                in0=turns[:].rearrange("p g (t c) -> p (g t) c", c=P)[:, :, 0:WRAP],
-                scalar1=-1.0,
-                scalar2=ROUND_MAGIC,
+                in0=freq[:, :, 0:WRAP],
+                scalar1=pos[:, a : a + 1],
+                scalar2=0.0,
                 op0=ALU.mult,
                 op1=ALU.add,
             )
-            turns_of[a] = (turns, whole)
+            whole_of[a] = whole
 
-        def timing_wrap(a):
-            turns, whole = turns_of[a]
-            wrapped = turns[:].rearrange("p g (t c) -> p (g t) c", c=P)[:, :, 0:WRAP]
+        def timing_reduce(a):
+            reduced = phase.tile([P, PACK, WRAP], F32)
             nc.vector.scalar_tensor_tensor(
-                out=wrapped, in0=whole[:], scalar=ROUND_MAGIC, in1=wrapped, op0=ALU.subtract, op1=ALU.add
+                out=reduced[:],
+                in0=freq[:, :, 0:WRAP],
+                scalar=pos[:, a : a + 1],
+                in1=whole_of[a][:],
+                op0=ALU.mult,
+                op1=ALU.subtract,
             )
+            reduced_of[a] = reduced
+
+        def timing_cosine(a):
+            reduced = reduced_of[a]
+            folded = phase.tile([P, PACK, WRAP], F32)
+            nc.vector.scalar_tensor_tensor(
+                out=folded[:], in0=reduced[:], scalar=0.25, in1=reduced[:], op0=ALU.is_gt, op1=ALU.subtract
+            )
+            folded_of[a] = folded
 
         def timing_signal(a):
-            turns, whole = turns_of[a]
-            signal = phase.tile([P, PASSES, HALF], F32)
-            nc.scalar.activation(out=signal[:], in_=turns[:], func=ACT.Sin, scale=2.0 * math.pi)
+            signal = phase.tile([P, PASSES, PACK, P], F32)
+            turn_rad = 2.0 * math.pi
+            quarter = math.pi / 2.0
+            nc.scalar.activation(out=signal[:, 0, :, 0:WRAP], in_=reduced_of[a][:], func=ACT.Sin, scale=turn_rad)
+            nc.scalar.activation(
+                out=signal[:, 1, :, 0:WRAP], in_=folded_of[a][:], func=ACT.Sin, scale=-turn_rad, bias=quarter
+            )
+            for g in range(PASSES):
+                nc.scalar.activation(
+                    out=signal[:, g, :, WRAP:P],
+                    in_=freq[:, :, WRAP:P],
+                    func=ACT.Sin,
+                    scale=pos_rad[:, a : a + 1],
+                    bias=quarter * g,
+                )
             timing[a] = signal
 
-        timing_turns(0)
-        timing_turns(1)
+        timing_whole(0)
+        timing_whole(1)
 
         w_perm = keep.tile([P, PASSES, PACK, P], BF16)
         nc.vector.tensor_copy(out=w_perm[:], in_=w_raw[:].rearrange("f (g p t) -> f g t p", g=PASSES, t=PACK))
         vec_f = keep.tile([P, 3, BLOCKS], F32)
         nc.vector.tensor_copy(out=vec_f[:], in_=vec_bf[:, :, 0:BLOCKS])
 
-        timing_wrap(0)
-        timing_wrap(1)
+        for a in (0, 1):
+            timing_reduce(a)
+            timing_cosine(a)
 
         xT = keep.tile([P, BATCH, GROUPS, P], BF16)
 
@@ -245,7 +263,7 @@ def tile_ffnn_encoder_pa_t_kernel(
                     out=e_of[a][:, b, g * HALF : (g + 1) * HALF],
                     in0=z_of[j][g][:],
                     scalar=0.0,
-                    in1=timing[a][:, g, :],
+                    in1=timing[a][:, g, :, :].rearrange("p t c -> p (t c)"),
                     op0=ALU.max,
                     op1=ALU.add,
                     accum_out=sum_of[a][:, b, g : g + 1],
@@ -422,6 +440,8 @@ def tile_ffnn_encoder_pa_t_kernel(
             if turn % BATCH == 1 and in_range(turn + 3):
                 timing_signal((turn + 3) // BATCH)
             if turn % BATCH == 1 and in_range(turn + 7):
-                timing_turns((turn + 7) // BATCH)
+                timing_whole((turn + 7) // BATCH)
+            if turn % BATCH == 2 and in_range(turn + 6):
+                timing_reduce((turn + 6) // BATCH)
             if turn % BATCH == 3 and in_range(turn + 5):
-                timing_wrap((turn + 5) // BATCH)
+                timing_cosine((turn + 5) // BATCH)

@@ -26,6 +26,7 @@ HALF = P * PACK
 BLOCKS = PASSES * PACK
 GROUPS = SEQ // P
 TILES = GROUPS * BATCH
+PAIR = 2
 EPS = 1e-3
 DECAY = math.exp(-math.log(10000.0) / 511.0)
 FIRST_SMALL = math.ceil(511.0 * math.log(2.0 * (SEQ - 1) / math.pi) / math.log(10000.0))
@@ -65,6 +66,7 @@ def tile_ffnn_encoder_pa_t_kernel(
     with ExitStack() as stack:
         keep = stack.enter_context(tc.tile_pool(name="keep", bufs=1))
         phase = stack.enter_context(tc.tile_pool(name="phase", bufs=2))
+        ahead_pool = stack.enter_context(tc.tile_pool(name="ahead", bufs=6))
         rows = stack.enter_context(tc.tile_pool(name="rows", bufs=3))
         small = stack.enter_context(tc.tile_pool(name="small", bufs=3))
         cols = stack.enter_context(tc.tile_pool(name="cols", bufs=2))
@@ -73,66 +75,61 @@ def tile_ffnn_encoder_pa_t_kernel(
         psum_t = stack.enter_context(tc.psum_pool(name="psum_t", bufs=2))
         stack.enter_context(tc.manual_schedule())
 
-        x_sb = keep.tile([P, BATCH, GROUPS * FIN], BF16)
+        first = PAIR * FIN
+        x_first = keep.tile([P, BATCH, first], BF16)
+        x_rest = keep.tile([P, BATCH, GROUPS * FIN - first], BF16)
         w_raw = keep.tile([P, D], BF16)
-        for b in range(BATCH):
-            nc.sync.dma_start(out=x_sb[:, b, :], in_=x[b].rearrange("(p a) f -> p (a f)", a=GROUPS))
-            if b == 0:
-                nc.sync.dma_start(out=w_raw[:], in_=W_emb)
+        x_rows = x.rearrange("b (p a) f -> p b (a f)", a=GROUPS)
+        nc.sync.dma_start(out=x_first[:], in_=x_rows[:, :, 0:first])
+        nc.sync.dma_start(out=w_raw[:], in_=W_emb)
+        nc.sync.dma_start(out=x_rest[:], in_=x_rows[:, :, first : GROUPS * FIN])
         vec_bf = keep.tile([P, 3, 16], BF16)
         for i, vec in enumerate((b_emb, g0, beta0)):
             nc.scalar.dma_start(
                 out=vec_bf[:, i, 0:BLOCKS].rearrange("p (g t) -> p g t", t=PACK),
                 in_=vec.rearrange("(g p t) -> p g t", g=PASSES, t=PACK),
             )
+        one = keep.tile([P, 1], F32)
+        nc.vector.memset(one[:], 1.0)
+        freq = keep.tile([P, PACK, P], F32)
+        for t in range(PACK):
+            nc.vector.tensor_scalar(
+                out=freq[:, t, 0:1], in0=one[:], scalar1=DECAY**t / (2.0 * math.pi), scalar2=None, op0=ALU.mult
+            )
+        n = 1
+        while n < P:
+            for m in range(n, min(4 * n, P), n):
+                nc.vector.tensor_scalar(
+                    out=freq[:, :, m : m + n],
+                    in0=freq[:, :, 0:n],
+                    scalar1=DECAY ** (PACK * m),
+                    scalar2=None,
+                    op0=ALU.mult,
+                )
+            n *= 4
+        pos = keep.tile([P, GROUPS], F32)
+        nc.gpsimd.iota(
+            pos[:], pattern=[[1, GROUPS]], base=0, channel_multiplier=GROUPS, allow_small_or_imprecise_dtypes=True
+        )
+        ident_bf = keep.tile([P, P], BF16)
+        make_identity(nc, ident_bf[:])
+        warm = keep.tile([P, 1], F32)
+        nc.scalar.activation(out=warm[:], in_=one[:], func=ACT.Sin)
+        pos_rad = keep.tile([P, GROUPS], F32)
+        nc.vector.tensor_scalar(out=pos_rad[:], in0=pos[:], scalar1=2.0 * math.pi, scalar2=None, op0=ALU.mult)
+        neg_half = keep.tile([P, BATCH], F32)
+        nc.vector.memset(neg_half[:], -0.5)
+
         w_codes = keep.tile([P, PASSES, N3], U32, align_bytes=64)
         w_planes = keep.tile([P, PASSES, N3], U8, align_bytes=64)
-        nc.vector.memset(w_planes[:].rearrange("p g n -> p (g n)").bitcast(I32), 0)
         weights = ((Wq_words, Wq_scales, bq), (Wk_words, Wk_scales, bk), (Wv_words, Wv_scales, bv))
         for j, (words, scales, bias) in enumerate(weights):
             nc.sync.dma_start(
                 out=w_codes[:, :, j * NOUT : (j + 1) * NOUT].bitcast(I32),
                 in_=words.rearrange("g p n t -> p g (n t)").bitcast(I32),
             )
-        for j, (words, scales, bias) in enumerate(weights):
-            for quad in range(4):
-                nc.sync.dma_start(
-                    out=w_planes[32 * quad : 32 * quad + 4, :, j * NOUT : (j + 1) * NOUT].bitcast(I32),
-                    in_=scales.bitcast(I32)[:, 4 * quad : 4 * quad + 4, :].rearrange("g r n -> r g n"),
-                )
-        bias_bc = keep.tile([P, N3], BF16)
-        for j, (words, scales, bias) in enumerate(weights):
-            nc.sync.dma_start(out=bias_bc[:, j * NOUT : (j + 1) * NOUT], in_=bias.partition_broadcast(P))
 
-        pos_i = keep.tile([P, GROUPS], I32)
-        nc.gpsimd.iota(pos_i[:], pattern=[[1, GROUPS]], base=0, channel_multiplier=GROUPS)
-        ident_bf = keep.tile([P, P], BF16)
-        make_identity(nc, ident_bf[:])
-        ident_f = keep.tile([P, P], F32)
-        make_identity(nc, ident_f[:])
-        neg_half = keep.tile([P, BATCH], F32)
-        nc.vector.memset(neg_half[:], -0.5)
-        warm = keep.tile([P, 1], F32)
-        nc.scalar.activation(out=warm[:], in_=neg_half[:, 0:1], func=ACT.Sin)
-
-        power = keep.tile([P, P], F32)
-        nc.vector.memset(power[:, 0:1], 1.0)
-        n = 1
-        while n < P:
-            nc.vector.tensor_scalar(
-                out=power[:, n : 2 * n], in0=power[:, 0:n], scalar1=DECAY ** (PACK * n), scalar2=None, op0=ALU.mult
-            )
-            n *= 2
-        freq = keep.tile([P, PACK, P], F32)
-        for t in range(PACK):
-            nc.vector.tensor_scalar(
-                out=freq[:, t, :], in0=power[:], scalar1=DECAY**t / (2.0 * math.pi), scalar2=None, op0=ALU.mult
-            )
-        pos = keep.tile([P, GROUPS], F32)
-        nc.vector.tensor_copy(out=pos[:], in_=pos_i[:])
-        pos_rad = keep.tile([P, GROUPS], F32)
-        nc.vector.tensor_scalar(out=pos_rad[:], in0=pos[:], scalar1=2.0 * math.pi, scalar2=None, op0=ALU.mult)
-
+        xt_of = {}
         whole_of = {}
         reduced_of = {}
         folded_of = {}
@@ -152,9 +149,9 @@ def tile_ffnn_encoder_pa_t_kernel(
         planes_of = {}
         acc_of = {}
 
-        def timing_whole(a):
+        def timing_whole(a, engine):
             whole = phase.tile([P, PACK, WRAP], I32)
-            nc.gpsimd.tensor_scalar(
+            engine.tensor_scalar(
                 out=whole[:],
                 in0=freq[:, :, 0:WRAP],
                 scalar1=pos[:, a : a + 1],
@@ -165,7 +162,7 @@ def tile_ffnn_encoder_pa_t_kernel(
             whole_of[a] = whole
 
         def timing_reduce(a):
-            reduced = phase.tile([P, PACK, WRAP], F32)
+            reduced = ahead_pool.tile([P, PACK, WRAP], F32)
             nc.vector.scalar_tensor_tensor(
                 out=reduced[:],
                 in0=freq[:, :, 0:WRAP],
@@ -178,7 +175,7 @@ def tile_ffnn_encoder_pa_t_kernel(
 
         def timing_cosine(a):
             reduced = reduced_of[a]
-            folded = phase.tile([P, PACK, WRAP], F32)
+            folded = ahead_pool.tile([P, PACK, WRAP], F32)
             nc.vector.scalar_tensor_tensor(
                 out=folded[:], in0=reduced[:], scalar=0.25, in1=reduced[:], op0=ALU.is_gt, op1=ALU.subtract
             )
@@ -202,30 +199,17 @@ def tile_ffnn_encoder_pa_t_kernel(
                 )
             timing[a] = signal
 
-        timing_whole(0)
-        timing_whole(1)
+        xT = keep.tile([P, GROUPS // PAIR, BATCH * PAIR, P], BF16)
 
-        w_perm = keep.tile([P, PASSES, PACK, P], BF16)
-        nc.vector.tensor_copy(out=w_perm[:], in_=w_raw[:].rearrange("f (g p t) -> f g t p", g=PASSES, t=PACK))
-        vec_f = keep.tile([P, 3, BLOCKS], F32)
-        nc.vector.tensor_copy(out=vec_f[:], in_=vec_bf[:, :, 0:BLOCKS])
-
-        for a in (0, 1):
-            timing_reduce(a)
-            timing_cosine(a)
-
-        xT = keep.tile([P, BATCH, GROUPS, P], BF16)
-
-        def transpose_x(b):
-            xt_ps = psum_z.tile([P, GROUPS, P], BF16, tag="z")
-            for a in range(GROUPS):
-                nc.tensor.transpose(xt_ps[:, a, :], x_sb[:, b, a * FIN : (a + 1) * FIN], ident_bf[:])
-            nc.scalar.copy(out=xT[:, b, :, :], in_=xt_ps[:])
+        def transpose_x(q):
+            xt_ps = psum_z.tile([P, BATCH * PAIR, P], BF16, tag="z")
+            for b in range(BATCH):
+                for a in range(PAIR):
+                    rows_x = x_first[:, b, :] if q == 0 else x_rest[:, b, (q - 1) * first : q * first]
+                    nc.tensor.transpose(xt_ps[:, b * PAIR + a, :], rows_x[:, a * FIN : (a + 1) * FIN], ident_bf[:])
+            xt_of[q] = xt_ps
 
         def embed_bias(j):
-            a, b = divmod(j, BATCH)
-            if a == 0:
-                transpose_x(b)
             banks = []
             for g in range(PASSES):
                 z = psum_z.tile([P, HALF], F32, tag="z")
@@ -246,7 +230,7 @@ def tile_ffnn_encoder_pa_t_kernel(
             a, b = divmod(j, BATCH)
             nc.tensor.matmul(
                 out=z_of[j][g][:],
-                lhsT=xT[:, b, a, :],
+                lhsT=xT[:, a // PAIR, b * PAIR + a % PAIR, :],
                 rhs=w_perm[:, g, :, :].rearrange("f t p -> f (t p)"),
                 start=False,
                 stop=True,
@@ -306,7 +290,7 @@ def tile_ffnn_encoder_pa_t_kernel(
             a, b = divmod(j, BATCH)
             if b == 0:
                 n_of[a] = rows.tile([P, BATCH, D], F32, name="normed")
-            if b == 0 or (b == 2 and j + LAG_NORM < LAG_PROJECT) or LAG_SCALE <= j + LAG_NORM < LAG_PACK:
+            if b in (0, 2) or LAG_SCALE <= j + LAG_NORM < LAG_PACK:
                 nc.vector.tensor_scalar(
                     out=n_of[a][:, b, :],
                     in0=e_of[a][:, b, :],
@@ -407,10 +391,35 @@ def tile_ffnn_encoder_pa_t_kernel(
         def in_range(j):
             return 0 <= j < TILES
 
+        timing_whole(0, nc.vector)
+        ident_f = keep.tile([P, P], F32)
+        make_identity(nc, ident_f[:])
+        timing_whole(1, nc.gpsimd)
+        timing_reduce(0)
+        nc.vector.memset(w_planes[:].rearrange("p g n -> p (g n)").bitcast(I32), 0)
+        timing_cosine(0)
+        timing_signal(0)
+        vec_f = keep.tile([P, 3, BLOCKS], F32)
+        nc.vector.tensor_copy(out=vec_f[:], in_=vec_bf[:, :, 0:BLOCKS])
+        transpose_x(0)
+        nc.vector.tensor_copy(out=xT[:, 0, :, :], in_=xt_of[0][:])
+        w_perm = keep.tile([P, PASSES, PACK, P], BF16)
+        nc.vector.tensor_copy(out=w_perm[:], in_=w_raw[:].rearrange("f (g p t) -> f g t p", g=PASSES, t=PACK))
         embed_bias(0)
         embed_matmul(0, 0)
         embed_matmul(0, 1)
-        timing_signal(0)
+        timing_reduce(1)
+
+        for j, (words, scales, bias) in enumerate(weights):
+            for quad in range(4):
+                nc.sync.dma_start(
+                    out=w_planes[32 * quad : 32 * quad + 4, :, j * NOUT : (j + 1) * NOUT].bitcast(I32),
+                    in_=scales.bitcast(I32)[:, 4 * quad : 4 * quad + 4, :].rearrange("g r n -> r g n"),
+                )
+        bias_bc = keep.tile([P, N3], BF16)
+        for j, (words, scales, bias) in enumerate(weights):
+            nc.sync.dma_start(out=bias_bc[:, j * NOUT : (j + 1) * NOUT], in_=bias.partition_broadcast(P))
+
         for turn in range(TILES + LAG_STORE):
             if in_range(turn + 1):
                 embed_bias(turn + 1)
@@ -419,6 +428,8 @@ def tile_ffnn_encoder_pa_t_kernel(
                 project_matmuls(turn - LAG_PROJECT)
             if in_range(turn + 1):
                 embed_matmul(turn + 1, 1)
+            if turn in (5, 9, 13):
+                nc.scalar.copy(out=xT[:, turn // 4, :, :], in_=xt_of[turn // 4][:])
             if in_range(turn):
                 embed_rows(turn)
                 if turn % BATCH == BATCH - 1:
@@ -431,17 +442,21 @@ def tile_ffnn_encoder_pa_t_kernel(
                 scale_blocks(turn - LAG_SCALE)
             if in_range(turn - LAG_TRANSPOSE):
                 transpose_blocks(turn - LAG_TRANSPOSE)
+            if turn in (4, 8, 12):
+                transpose_x(turn // 4)
             if in_range(turn - LAG_STORE):
                 project_store(turn - LAG_STORE)
             if in_range(turn - LAG_NORM):
                 normalise(turn - LAG_NORM)
             if in_range(turn - LAG_PACK):
                 pack(turn - LAG_PACK)
+            ahead, piece = divmod(turn, 2)
+            if piece == 0:
+                if ahead + 2 < GROUPS:
+                    timing_whole(ahead + 2, nc.gpsimd)
+                if ahead + 1 < GROUPS:
+                    timing_cosine(ahead + 1)
+            elif ahead + 2 < GROUPS:
+                timing_reduce(ahead + 2)
             if turn % BATCH == 1 and in_range(turn + 3):
                 timing_signal((turn + 3) // BATCH)
-            if turn % BATCH == 1 and in_range(turn + 7):
-                timing_whole((turn + 7) // BATCH)
-            if turn % BATCH == 2 and in_range(turn + 6):
-                timing_reduce((turn + 6) // BATCH)
-            if turn % BATCH == 3 and in_range(turn + 5):
-                timing_cosine((turn + 5) // BATCH)

@@ -29,8 +29,10 @@ TILES = GROUPS * BATCH
 PAIR = 2
 EPS = 1e-3
 DECAY = math.exp(-math.log(10000.0) / 511.0)
-FIRST_SMALL = math.ceil(511.0 * math.log(2.0 * (SEQ - 1) / math.pi) / math.log(10000.0))
+FIRST_SMALL = math.ceil(511.0 * math.log((SEQ - 1) / (1.5 * math.pi)) / math.log(10000.0))
 WRAP = -(-FIRST_SMALL // PACK)
+
+EARLY = 2
 
 LAG_NORM = 5
 LAG_TRANSPOSE = 9
@@ -66,11 +68,10 @@ def tile_ffnn_encoder_pa_t_kernel(
     with ExitStack() as stack:
         keep = stack.enter_context(tc.tile_pool(name="keep", bufs=1))
         phase = stack.enter_context(tc.tile_pool(name="phase", bufs=2))
-        ahead_pool = stack.enter_context(tc.tile_pool(name="ahead", bufs=6))
         rows = stack.enter_context(tc.tile_pool(name="rows", bufs=3))
         small = stack.enter_context(tc.tile_pool(name="small", bufs=3))
         cols = stack.enter_context(tc.tile_pool(name="cols", bufs=2))
-        results = stack.enter_context(tc.tile_pool(name="results", bufs=4))
+        results = stack.enter_context(tc.tile_pool(name="results", bufs=6))
         psum_z = stack.enter_context(tc.psum_pool(name="psum_z", bufs=6))
         psum_t = stack.enter_context(tc.psum_pool(name="psum_t", bufs=2))
         stack.enter_context(tc.manual_schedule())
@@ -80,15 +81,20 @@ def tile_ffnn_encoder_pa_t_kernel(
         x_rest = keep.tile([P, BATCH, GROUPS * FIN - first], BF16)
         w_raw = keep.tile([P, D], BF16)
         x_rows = x.rearrange("b (p a) f -> p b (a f)", a=GROUPS)
-        nc.sync.dma_start(out=x_first[:], in_=x_rows[:, :, 0:first])
-        nc.sync.dma_start(out=w_raw[:], in_=W_emb)
-        nc.sync.dma_start(out=x_rest[:], in_=x_rows[:, :, first : GROUPS * FIN])
         vec_bf = keep.tile([P, 3, 16], BF16)
-        for i, vec in enumerate((b_emb, g0, beta0)):
-            nc.scalar.dma_start(
+
+        def load_vector(i, vec):
+            nc.sync.dma_start(
                 out=vec_bf[:, i, 0:BLOCKS].rearrange("p (g t) -> p g t", t=PACK),
                 in_=vec.rearrange("(g p t) -> p g t", g=PASSES, t=PACK),
             )
+
+        nc.sync.dma_start(out=x_first[:], in_=x_rows[:, :, 0:first])
+        load_vector(0, b_emb)
+        nc.sync.dma_start(out=w_raw[:], in_=W_emb)
+        nc.sync.dma_start(out=x_rest[:], in_=x_rows[:, :, first : GROUPS * FIN])
+        load_vector(1, g0)
+        load_vector(2, beta0)
         one = keep.tile([P, 1], F32)
         nc.vector.memset(one[:], 1.0)
         freq = keep.tile([P, PACK, P], F32)
@@ -111,12 +117,14 @@ def tile_ffnn_encoder_pa_t_kernel(
         nc.gpsimd.iota(
             pos[:], pattern=[[1, GROUPS]], base=0, channel_multiplier=GROUPS, allow_small_or_imprecise_dtypes=True
         )
+        ident_f = keep.tile([P, P], F32)
+        make_identity(nc, ident_f[:])
         ident_bf = keep.tile([P, P], BF16)
-        make_identity(nc, ident_bf[:])
+        nc.vector.tensor_copy(out=ident_bf[:], in_=ident_f[:])
         warm = keep.tile([P, 1], F32)
         nc.scalar.activation(out=warm[:], in_=one[:], func=ACT.Sin)
-        pos_rad = keep.tile([P, GROUPS], F32)
-        nc.vector.tensor_scalar(out=pos_rad[:], in0=pos[:], scalar1=2.0 * math.pi, scalar2=None, op0=ALU.mult)
+        neg_rad = keep.tile([P, GROUPS], F32)
+        nc.vector.tensor_scalar(out=neg_rad[:], in0=pos[:], scalar1=-2.0 * math.pi, scalar2=None, op0=ALU.mult)
         neg_half = keep.tile([P, BATCH], F32)
         nc.vector.memset(neg_half[:], -0.5)
 
@@ -150,7 +158,7 @@ def tile_ffnn_encoder_pa_t_kernel(
         acc_of = {}
 
         def timing_whole(a, engine):
-            whole = phase.tile([P, PACK, WRAP], I32)
+            whole = phase.tile([P, PACK, WRAP], I32, bufs=EARLY + 1)
             engine.tensor_scalar(
                 out=whole[:],
                 in0=freq[:, :, 0:WRAP],
@@ -162,7 +170,7 @@ def tile_ffnn_encoder_pa_t_kernel(
             whole_of[a] = whole
 
         def timing_reduce(a):
-            reduced = ahead_pool.tile([P, PACK, WRAP], F32)
+            reduced = phase.tile([P, PACK, WRAP], F32, bufs=EARLY + 1)
             nc.vector.scalar_tensor_tensor(
                 out=reduced[:],
                 in0=freq[:, :, 0:WRAP],
@@ -175,28 +183,28 @@ def tile_ffnn_encoder_pa_t_kernel(
 
         def timing_cosine(a):
             reduced = reduced_of[a]
-            folded = ahead_pool.tile([P, PACK, WRAP], F32)
+            folded = phase.tile([P, PACK, WRAP], F32, bufs=EARLY + 1)
             nc.vector.scalar_tensor_tensor(
                 out=folded[:], in0=reduced[:], scalar=0.25, in1=reduced[:], op0=ALU.is_gt, op1=ALU.subtract
             )
             folded_of[a] = folded
 
         def timing_signal(a):
-            signal = phase.tile([P, PASSES, PACK, P], F32)
+            signal = phase.tile([P, PASSES, PACK, P], F32, bufs=EARLY + 1)
             turn_rad = 2.0 * math.pi
             quarter = math.pi / 2.0
             nc.scalar.activation(out=signal[:, 0, :, 0:WRAP], in_=reduced_of[a][:], func=ACT.Sin, scale=turn_rad)
-            nc.scalar.activation(
-                out=signal[:, 1, :, 0:WRAP], in_=folded_of[a][:], func=ACT.Sin, scale=-turn_rad, bias=quarter
-            )
             for g in range(PASSES):
                 nc.scalar.activation(
                     out=signal[:, g, :, WRAP:P],
                     in_=freq[:, :, WRAP:P],
                     func=ACT.Sin,
-                    scale=pos_rad[:, a : a + 1],
-                    bias=quarter * g,
+                    scale=neg_rad[:, a : a + 1],
+                    bias=(math.pi, quarter)[g],
                 )
+            nc.scalar.activation(
+                out=signal[:, 1, :, 0:WRAP], in_=folded_of[a][:], func=ACT.Sin, scale=-turn_rad, bias=quarter
+            )
             timing[a] = signal
 
         xT = keep.tile([P, GROUPS // PAIR, BATCH * PAIR, P], BF16)
@@ -217,7 +225,7 @@ def tile_ffnn_encoder_pa_t_kernel(
                     c = g * PACK + t
                     nc.tensor.matmul(
                         out=z[:, t * P : (t + 1) * P],
-                        lhsT=vec_f[:, 0, c : c + 1].to_broadcast([P, P]),
+                        lhsT=bias_f[:, c : c + 1].to_broadcast([P, P]),
                         rhs=ident_f[:],
                         is_transpose=True,
                         start=(t == 0),
@@ -290,7 +298,7 @@ def tile_ffnn_encoder_pa_t_kernel(
             a, b = divmod(j, BATCH)
             if b == 0:
                 n_of[a] = rows.tile([P, BATCH, D], F32, name="normed")
-            if b in (0, 2) or LAG_SCALE <= j + LAG_NORM < LAG_PACK:
+            if b == 0 or (b == 2 and j + LAG_NORM < LAG_PROJECT) or LAG_SCALE <= j + LAG_NORM < LAG_PACK:
                 nc.vector.tensor_scalar(
                     out=n_of[a][:, b, :],
                     in0=e_of[a][:, b, :],
@@ -326,8 +334,8 @@ def tile_ffnn_encoder_pa_t_kernel(
                     out=ht_of[a, g][:, t, :],
                     in_=nt_of[a, c][:].rearrange("p b k -> p (b k)"),
                     func=ACT.Identity,
-                    scale=vec_f[:, 1, c : c + 1],
-                    bias=vec_f[:, 2, c : c + 1],
+                    scale=affine_f[:, 0, c : c + 1],
+                    bias=affine_f[:, 1, c : c + 1],
                 )
 
         def pack(m):
@@ -391,24 +399,29 @@ def tile_ffnn_encoder_pa_t_kernel(
         def in_range(j):
             return 0 <= j < TILES
 
-        timing_whole(0, nc.vector)
-        ident_f = keep.tile([P, P], F32)
-        make_identity(nc, ident_f[:])
-        timing_whole(1, nc.gpsimd)
-        timing_reduce(0)
-        nc.vector.memset(w_planes[:].rearrange("p g n -> p (g n)").bitcast(I32), 0)
+        for a in range(EARLY):
+            timing_whole(a, nc.vector)
+        for a in range(EARLY):
+            timing_reduce(a)
         timing_cosine(0)
+        bias_f = keep.tile([P, BLOCKS], F32)
+        nc.vector.tensor_copy(out=bias_f[:], in_=vec_bf[:, 0, 0:BLOCKS])
+        for a in range(1, EARLY):
+            timing_cosine(a)
         timing_signal(0)
-        vec_f = keep.tile([P, 3, BLOCKS], F32)
-        nc.vector.tensor_copy(out=vec_f[:], in_=vec_bf[:, :, 0:BLOCKS])
+        timing_whole(EARLY, nc.gpsimd)
         transpose_x(0)
-        nc.vector.tensor_copy(out=xT[:, 0, :, :], in_=xt_of[0][:])
+        nc.scalar.copy(out=xT[:, 0, :, :], in_=xt_of[0][:])
+        for a in range(1, EARLY):
+            timing_signal(a)
         w_perm = keep.tile([P, PASSES, PACK, P], BF16)
         nc.vector.tensor_copy(out=w_perm[:], in_=w_raw[:].rearrange("f (g p t) -> f g t p", g=PASSES, t=PACK))
+        timing_reduce(EARLY)
         embed_bias(0)
         embed_matmul(0, 0)
         embed_matmul(0, 1)
-        timing_reduce(1)
+        nc.vector.memset(w_planes[:].rearrange("p g n -> p (g n)").bitcast(I32), 0)
+        affine_f = keep.tile([P, 2, BLOCKS], F32)
 
         for j, (words, scales, bias) in enumerate(weights):
             for quad in range(4):
@@ -450,13 +463,18 @@ def tile_ffnn_encoder_pa_t_kernel(
                 normalise(turn - LAG_NORM)
             if in_range(turn - LAG_PACK):
                 pack(turn - LAG_PACK)
-            ahead, piece = divmod(turn, 2)
-            if piece == 0:
-                if ahead + 2 < GROUPS:
-                    timing_whole(ahead + 2, nc.gpsimd)
-                if ahead + 1 < GROUPS:
-                    timing_cosine(ahead + 1)
-            elif ahead + 2 < GROUPS:
-                timing_reduce(ahead + 2)
-            if turn % BATCH == 1 and in_range(turn + 3):
+            if turn == BATCH:
+                nc.vector.tensor_copy(out=affine_f[:], in_=vec_bf[:, 1:3, 0:BLOCKS])
+            if turn == 0:
+                timing_cosine(EARLY)
+            if turn == 1:
+                timing_signal(EARLY)
+            late = range((EARLY + 1) * BATCH, TILES)
+            if turn % BATCH == 1 and turn + 3 in late:
                 timing_signal((turn + 3) // BATCH)
+            if turn % BATCH == 1 and turn + 7 in late:
+                timing_whole((turn + 7) // BATCH, nc.gpsimd)
+            if turn % BATCH == 2 and turn + 6 in late:
+                timing_reduce((turn + 6) // BATCH)
+            if turn % BATCH == 3 and turn + 5 in late:
+                timing_cosine((turn + 5) // BATCH)

@@ -119,8 +119,6 @@ def tile_ffnn_encoder_pa_t_kernel(
         )
         ident_f = keep.tile([P, P], F32)
         make_identity(nc, ident_f[:])
-        ident_bf = keep.tile([P, P], BF16)
-        nc.vector.tensor_copy(out=ident_bf[:], in_=ident_f[:])
         warm = keep.tile([P, 1], F32)
         nc.scalar.activation(out=warm[:], in_=one[:], func=ACT.Sin)
         neg_rad = keep.tile([P, GROUPS], F32)
@@ -298,7 +296,11 @@ def tile_ffnn_encoder_pa_t_kernel(
             a, b = divmod(j, BATCH)
             if b == 0:
                 n_of[a] = rows.tile([P, BATCH, D], F32, name="normed")
-            if b == 0 or (b == 2 and j + LAG_NORM < LAG_PROJECT) or LAG_SCALE <= j + LAG_NORM < LAG_PACK:
+            if (
+                b == 0
+                or (b == 2 and j + LAG_NORM < LAG_PROJECT)
+                or (b == 1 and LAG_SCALE <= j + LAG_NORM <= LAG_STORE + 1)
+            ):
                 nc.vector.tensor_scalar(
                     out=n_of[a][:, b, :],
                     in0=e_of[a][:, b, :],
@@ -346,7 +348,9 @@ def tile_ffnn_encoder_pa_t_kernel(
                 planes_of[a] = cols.tile([P, PASSES, BATCH * P], U8, name="planes", align_bytes=64)
             if not quantise:
                 grouped = cols.tile([P, BATCH * P, PACK], BF16, align_bytes=64)
-                mine = (BATCH - 1) * P if m + LAG_PACK >= TILES + LAG_NORM else BATCH * P
+                mine = BATCH * P
+                if m + LAG_PACK >= TILES + LAG_NORM:
+                    mine -= (2 if m == TILES - 2 else 1) * P
                 nc.vector.tensor_copy(
                     out=grouped[:, 0:mine, :].rearrange("p (c i) t -> p c t i", i=4),
                     in_=ht_of[a, g][:, :, 0:mine].rearrange("p t (c i) -> p c t i", i=4),
@@ -399,17 +403,18 @@ def tile_ffnn_encoder_pa_t_kernel(
         def in_range(j):
             return 0 <= j < TILES
 
-        for a in range(EARLY):
+        for a in range(EARLY + 1):
             timing_whole(a, nc.vector)
         for a in range(EARLY):
             timing_reduce(a)
+        ident_bf = keep.tile([P, P], BF16)
+        nc.vector.tensor_copy(out=ident_bf[:], in_=ident_f[:])
         timing_cosine(0)
         bias_f = keep.tile([P, BLOCKS], F32)
         nc.vector.tensor_copy(out=bias_f[:], in_=vec_bf[:, 0, 0:BLOCKS])
         for a in range(1, EARLY):
             timing_cosine(a)
         timing_signal(0)
-        timing_whole(EARLY, nc.gpsimd)
         transpose_x(0)
         nc.scalar.copy(out=xT[:, 0, :, :], in_=xt_of[0][:])
         for a in range(1, EARLY):
@@ -417,21 +422,14 @@ def tile_ffnn_encoder_pa_t_kernel(
         w_perm = keep.tile([P, PASSES, PACK, P], BF16)
         nc.vector.tensor_copy(out=w_perm[:], in_=w_raw[:].rearrange("f (g p t) -> f g t p", g=PASSES, t=PACK))
         timing_reduce(EARLY)
+        timing_cosine(EARLY)
+        timing_signal(EARLY)
         embed_bias(0)
         embed_matmul(0, 0)
         embed_matmul(0, 1)
-        nc.vector.memset(w_planes[:].rearrange("p g n -> p (g n)").bitcast(I32), 0)
         affine_f = keep.tile([P, 2, BLOCKS], F32)
 
-        for j, (words, scales, bias) in enumerate(weights):
-            for quad in range(4):
-                nc.sync.dma_start(
-                    out=w_planes[32 * quad : 32 * quad + 4, :, j * NOUT : (j + 1) * NOUT].bitcast(I32),
-                    in_=scales.bitcast(I32)[:, 4 * quad : 4 * quad + 4, :].rearrange("g r n -> r g n"),
-                )
         bias_bc = keep.tile([P, N3], BF16)
-        for j, (words, scales, bias) in enumerate(weights):
-            nc.sync.dma_start(out=bias_bc[:, j * NOUT : (j + 1) * NOUT], in_=bias.partition_broadcast(P))
 
         for turn in range(TILES + LAG_STORE):
             if in_range(turn + 1):
@@ -464,11 +462,16 @@ def tile_ffnn_encoder_pa_t_kernel(
             if in_range(turn - LAG_PACK):
                 pack(turn - LAG_PACK)
             if turn == BATCH:
+                nc.vector.memset(w_planes[:].rearrange("p g n -> p (g n)").bitcast(I32), 0)
                 nc.vector.tensor_copy(out=affine_f[:], in_=vec_bf[:, 1:3, 0:BLOCKS])
-            if turn == 0:
-                timing_cosine(EARLY)
-            if turn == 1:
-                timing_signal(EARLY)
+                for j, (words, scales, bias) in enumerate(weights):
+                    for quad in range(4):
+                        nc.sync.dma_start(
+                            out=w_planes[32 * quad : 32 * quad + 4, :, j * NOUT : (j + 1) * NOUT].bitcast(I32),
+                            in_=scales.bitcast(I32)[:, 4 * quad : 4 * quad + 4, :].rearrange("g r n -> r g n"),
+                        )
+                for j, (words, scales, bias) in enumerate(weights):
+                    nc.sync.dma_start(out=bias_bc[:, j * NOUT : (j + 1) * NOUT], in_=bias.partition_broadcast(P))
             late = range((EARLY + 1) * BATCH, TILES)
             if turn % BATCH == 1 and turn + 3 in late:
                 timing_signal((turn + 3) // BATCH)

@@ -139,6 +139,7 @@ def tile_ffnn_encoder_pa_t_kernel(
         whole_of = {}
         reduced_of = {}
         folded_of = {}
+        gate_of = {}
         mean_of = {}
         timing = {}
         z_of = {}
@@ -292,31 +293,33 @@ def tile_ffnn_encoder_pa_t_kernel(
             scale_of[a] = rstd
             shift_of[a] = shift
 
+        def on_gpsimd(j):
+            return j % BATCH == 1 and BATCH <= j < TILES - BATCH
+
+        def release(j):
+            a, b = divmod(j, BATCH)
+            if on_gpsimd(j):
+                gate = small.tile([P, 1], F32)
+                nc.vector.tensor_copy(out=gate[:], in_=shift_of[a][:, b : b + 1])
+                gate_of[j] = gate
+
         def normalise(j):
             a, b = divmod(j, BATCH)
             if b == 0:
                 n_of[a] = rows.tile([P, BATCH, D], F32, name="normed")
-            if (
-                b == 0
-                or (b == 2 and j + LAG_NORM < LAG_PROJECT)
-                or (b == 1 and LAG_SCALE <= j + LAG_NORM <= LAG_STORE + 1)
-            ):
+            rows_in, rows_out = e_of[a][:, b, :], n_of[a][:, b, :]
+            scale, shift = scale_of[a][:, b : b + 1], shift_of[a][:, b : b + 1]
+            filling = j + LAG_NORM < LAG_PROJECT
+            if on_gpsimd(j):
+                nc.gpsimd.tensor_scalar(
+                    out=rows_out, in0=rows_in, scalar1=scale, scalar2=gate_of[j][:], op0=ALU.mult, op1=ALU.add
+                )
+            elif (b == 0 and (a < 4 or a % 2 == 1)) or (b == 2 and filling):
                 nc.vector.tensor_scalar(
-                    out=n_of[a][:, b, :],
-                    in0=e_of[a][:, b, :],
-                    scalar1=scale_of[a][:, b : b + 1],
-                    scalar2=shift_of[a][:, b : b + 1],
-                    op0=ALU.mult,
-                    op1=ALU.add,
+                    out=rows_out, in0=rows_in, scalar1=scale, scalar2=shift, op0=ALU.mult, op1=ALU.add
                 )
             else:
-                nc.scalar.activation(
-                    out=n_of[a][:, b, :],
-                    in_=e_of[a][:, b, :],
-                    func=ACT.Identity,
-                    scale=scale_of[a][:, b : b + 1],
-                    bias=shift_of[a][:, b : b + 1],
-                )
+                nc.scalar.activation(out=rows_out, in_=rows_in, func=ACT.Identity, scale=scale, bias=shift)
 
         def transpose_blocks(k):
             a, quarter = divmod(k, BATCH)
@@ -403,12 +406,12 @@ def tile_ffnn_encoder_pa_t_kernel(
         def in_range(j):
             return 0 <= j < TILES
 
+        ident_bf = keep.tile([P, P], BF16)
+        nc.vector.tensor_copy(out=ident_bf[:], in_=ident_f[:])
         for a in range(EARLY + 1):
             timing_whole(a, nc.vector)
         for a in range(EARLY):
             timing_reduce(a)
-        ident_bf = keep.tile([P, P], BF16)
-        nc.vector.tensor_copy(out=ident_bf[:], in_=ident_f[:])
         timing_cosine(0)
         bias_f = keep.tile([P, BLOCKS], F32)
         nc.vector.tensor_copy(out=bias_f[:], in_=vec_bf[:, 0, 0:BLOCKS])
@@ -441,6 +444,8 @@ def tile_ffnn_encoder_pa_t_kernel(
                 embed_matmul(turn + 1, 1)
             if turn in (5, 9, 13):
                 nc.scalar.copy(out=xT[:, turn // 4, :, :], in_=xt_of[turn // 4][:])
+            if in_range(turn - LAG_NORM):
+                release(turn - LAG_NORM)
             if in_range(turn):
                 embed_rows(turn)
                 if turn % BATCH == BATCH - 1:

@@ -139,7 +139,6 @@ def tile_ffnn_encoder_pa_t_kernel(
         whole_of = {}
         reduced_of = {}
         folded_of = {}
-        gate_of = {}
         mean_of = {}
         timing = {}
         z_of = {}
@@ -294,27 +293,31 @@ def tile_ffnn_encoder_pa_t_kernel(
             shift_of[a] = shift
 
         def on_gpsimd(j):
-            return j % BATCH == 1 and BATCH <= j < TILES - BATCH
-
-        def release(j):
             a, b = divmod(j, BATCH)
-            if on_gpsimd(j):
-                gate = small.tile([P, 1], F32)
-                nc.vector.tensor_copy(out=gate[:], in_=shift_of[a][:, b : b + 1])
-                gate_of[j] = gate
+            return 1 <= a < GROUPS - 1 and (b == 1 or (b == 2 and j + LAG_NORM >= LAG_PROJECT))
 
-        def normalise(j):
+        def normalise_early(j):
             a, b = divmod(j, BATCH)
             if b == 0:
                 n_of[a] = rows.tile([P, BATCH, D], F32, name="normed")
+            if on_gpsimd(j):
+                gate = small.tile([P, 1], F32)
+                nc.vector.tensor_copy(out=gate[:], in_=shift_of[a][:, b : b + 1])
+                nc.gpsimd.tensor_scalar(
+                    out=n_of[a][:, b, :],
+                    in0=e_of[a][:, b, :],
+                    scalar1=scale_of[a][:, b : b + 1],
+                    scalar2=gate[:],
+                    op0=ALU.mult,
+                    op1=ALU.add,
+                )
+
+        def normalise(j):
+            a, b = divmod(j, BATCH)
             rows_in, rows_out = e_of[a][:, b, :], n_of[a][:, b, :]
             scale, shift = scale_of[a][:, b : b + 1], shift_of[a][:, b : b + 1]
             filling = j + LAG_NORM < LAG_PROJECT
-            if on_gpsimd(j):
-                nc.gpsimd.tensor_scalar(
-                    out=rows_out, in0=rows_in, scalar1=scale, scalar2=gate_of[j][:], op0=ALU.mult, op1=ALU.add
-                )
-            elif (b == 0 and (a < 4 or a % 2 == 1)) or (b == 2 and filling):
+            if (filling and (b in (0, 2) or j == BATCH - 1)) or j == TILES - BATCH:
                 nc.vector.tensor_scalar(
                     out=rows_out, in0=rows_in, scalar1=scale, scalar2=shift, op0=ALU.mult, op1=ALU.add
                 )
@@ -389,16 +392,25 @@ def tile_ffnn_encoder_pa_t_kernel(
                     )
             acc_of[j] = (acc_qk, acc_v)
 
-        def project_store(j):
-            a, b = divmod(j, BATCH)
+        def add_bias(j):
             acc_qk, acc_v = acc_of[j]
             res = results.tile([P, N3], F32)
-            nc.vector.tensor_tensor(
-                out=res[:, 0 : 2 * NOUT], in0=acc_qk[:], in1=bias_bc[:, 0 : 2 * NOUT], op=ALU.add
-            )
-            nc.vector.tensor_tensor(out=res[:, 2 * NOUT : N3], in0=acc_v[:], in1=bias_bc[:, 2 * NOUT : N3], op=ALU.add)
+            for acc, n_cols in ((acc_qk, slice(0, 2 * NOUT)), (acc_v, slice(2 * NOUT, N3))):
+                nc.vector.tensor_tensor(out=res[:, n_cols], in0=acc[:], in1=bias_bc[:, n_cols], op=ALU.add)
+            store(j, res, nc.sync)
+
+        def add_bias_apart(j):
+            acc_qk, acc_v = acc_of[j]
+            res = results.tile([P, N3], F32)
+            for acc, n_cols in ((acc_qk, slice(0, 2 * NOUT)), (acc_v, slice(2 * NOUT, N3))):
+                nc.scalar.copy(out=res[:, n_cols], in_=acc[:])
+            nc.gpsimd.tensor_tensor(out=res[:], in0=res[:], in1=bias_bc[:], op=ALU.add)
+            store(j, res, nc.scalar)
+
+        def store(j, res, queue):
+            a, b = divmod(j, BATCH)
             for i, out in enumerate((out_0, out_1, out_2)):
-                nc.sync.dma_start(
+                queue.dma_start(
                     out=out[b].rearrange("(p a) n -> p a n", a=GROUPS)[:, a, :],
                     in_=res[:, i * NOUT : (i + 1) * NOUT],
                 )
@@ -445,7 +457,7 @@ def tile_ffnn_encoder_pa_t_kernel(
             if turn in (5, 9, 13):
                 nc.scalar.copy(out=xT[:, turn // 4, :, :], in_=xt_of[turn // 4][:])
             if in_range(turn - LAG_NORM):
-                release(turn - LAG_NORM)
+                normalise_early(turn - LAG_NORM)
             if in_range(turn):
                 embed_rows(turn)
                 if turn % BATCH == BATCH - 1:
@@ -461,8 +473,8 @@ def tile_ffnn_encoder_pa_t_kernel(
             if turn in (4, 8, 12):
                 transpose_x(turn // 4)
             if in_range(turn - LAG_STORE):
-                project_store(turn - LAG_STORE)
-            if in_range(turn - LAG_NORM):
+                (add_bias_apart if turn - LAG_STORE == TILES - BATCH else add_bias)(turn - LAG_STORE)
+            if in_range(turn - LAG_NORM) and not on_gpsimd(turn - LAG_NORM):
                 normalise(turn - LAG_NORM)
             if in_range(turn - LAG_PACK):
                 pack(turn - LAG_PACK)

@@ -294,7 +294,7 @@ def tile_ffnn_encoder_pa_t_kernel(
 
         def on_gpsimd(j):
             a, b = divmod(j, BATCH)
-            return 1 <= a < GROUPS - 1 and (b == 1 or (b == 2 and j + LAG_NORM >= LAG_PROJECT))
+            return 1 < j < TILES - BATCH and b in (1, 2)
 
         def normalise_early(j):
             a, b = divmod(j, BATCH)
@@ -317,7 +317,7 @@ def tile_ffnn_encoder_pa_t_kernel(
             rows_in, rows_out = e_of[a][:, b, :], n_of[a][:, b, :]
             scale, shift = scale_of[a][:, b : b + 1], shift_of[a][:, b : b + 1]
             filling = j + LAG_NORM < LAG_PROJECT
-            if (filling and (b in (0, 2) or j == BATCH - 1)) or j == TILES - BATCH:
+            if (filling and b == 0) or j in (BATCH - 1, TILES - BATCH):
                 nc.vector.tensor_scalar(
                     out=rows_out, in0=rows_in, scalar1=scale, scalar2=shift, op0=ALU.mult, op1=ALU.add
                 )
@@ -473,7 +473,7 @@ def tile_ffnn_encoder_pa_t_kernel(
             if turn in (4, 8, 12):
                 transpose_x(turn // 4)
             if in_range(turn - LAG_STORE):
-                (add_bias_apart if turn - LAG_STORE == TILES - BATCH else add_bias)(turn - LAG_STORE)
+                (add_bias_apart if turn - LAG_STORE == TILES - BATCH - 2 else add_bias)(turn - LAG_STORE)
             if in_range(turn - LAG_NORM) and not on_gpsimd(turn - LAG_NORM):
                 normalise(turn - LAG_NORM)
             if in_range(turn - LAG_PACK):

@@ -32,6 +32,7 @@ DECAY = math.exp(-math.log(10000.0) / 511.0)
 FIRST_SMALL = math.ceil(511.0 * math.log((SEQ - 1) / (1.5 * math.pi)) / math.log(10000.0))
 WRAP = -(-FIRST_SMALL // PACK)
 
+WARM_UPS = 4
 EARLY = 2
 
 LAG_NORM = 5
@@ -72,8 +73,8 @@ def tile_ffnn_encoder_pa_t_kernel(
         small = stack.enter_context(tc.tile_pool(name="small", bufs=3))
         cols = stack.enter_context(tc.tile_pool(name="cols", bufs=2))
         results = stack.enter_context(tc.tile_pool(name="results", bufs=6))
-        psum_z = stack.enter_context(tc.psum_pool(name="psum_z", bufs=6))
-        psum_t = stack.enter_context(tc.psum_pool(name="psum_t", bufs=2))
+        psum_z = stack.enter_context(tc.psum_pool(name="psum_z", bufs=5))
+        psum_t = stack.enter_context(tc.psum_pool(name="psum_t", bufs=3))
         stack.enter_context(tc.manual_schedule())
 
         first = PAIR * FIN
@@ -113,6 +114,13 @@ def tile_ffnn_encoder_pa_t_kernel(
                     op0=ALU.mult,
                 )
             n *= 4
+        zero = keep.tile([P, 1], BF16)
+        nc.gpsimd.memset(zero[:], 0.0)
+        for i in range(WARM_UPS):
+            idle = psum_z.tile([P, HALF], F32, tag="z")
+            nc.tensor.matmul(
+                out=idle[:], lhsT=zero[:].to_broadcast([P, P]), rhs=zero[:].to_broadcast([P, HALF]), start=True, stop=True
+            )
         pos = keep.tile([P, GROUPS], F32)
         nc.gpsimd.iota(
             pos[:], pattern=[[1, GROUPS]], base=0, channel_multiplier=GROUPS, allow_small_or_imprecise_dtypes=True
@@ -156,11 +164,11 @@ def tile_ffnn_encoder_pa_t_kernel(
         acc_of = {}
 
         def timing_whole(a, engine):
-            whole = phase.tile([P, PACK, WRAP], I32, bufs=EARLY + 1)
+            whole = phase.tile([P, PACK, WRAP], I32, bufs=GROUPS)
             engine.tensor_scalar(
                 out=whole[:],
                 in0=freq[:, :, 0:WRAP],
-                scalar1=pos[:, a : a + 1],
+                scalar1=(pos_late if a > EARLY else pos)[:, a : a + 1],
                 scalar2=0.0,
                 op0=ALU.mult,
                 op1=ALU.add,
@@ -284,7 +292,7 @@ def tile_ffnn_encoder_pa_t_kernel(
         def statistics(a):
             neg_mean, rest = mean_of[a]
             var = small.tile([P, BATCH], F32)
-            nc.gpsimd.tensor_tensor(out=var[:], in0=sq_of[a][:], in1=rest[:], op=ALU.add)
+            nc.vector.tensor_tensor(out=var[:], in0=sq_of[a][:], in1=rest[:], op=ALU.add)
             rstd = small.tile([P, BATCH], F32)
             nc.gpsimd.tensor_tensor(out=rstd[:], in0=var[:], in1=neg_half[:], op=ALU.pow)
             shift = small.tile([P, BATCH], F32)
@@ -397,20 +405,12 @@ def tile_ffnn_encoder_pa_t_kernel(
             res = results.tile([P, N3], F32)
             for acc, n_cols in ((acc_qk, slice(0, 2 * NOUT)), (acc_v, slice(2 * NOUT, N3))):
                 nc.vector.tensor_tensor(out=res[:, n_cols], in0=acc[:], in1=bias_bc[:, n_cols], op=ALU.add)
-            store(j, res, nc.sync)
+            store(j, res)
 
-        def add_bias_apart(j):
-            acc_qk, acc_v = acc_of[j]
-            res = results.tile([P, N3], F32)
-            for acc, n_cols in ((acc_qk, slice(0, 2 * NOUT)), (acc_v, slice(2 * NOUT, N3))):
-                nc.scalar.copy(out=res[:, n_cols], in_=acc[:])
-            nc.gpsimd.tensor_tensor(out=res[:], in0=res[:], in1=bias_bc[:], op=ALU.add)
-            store(j, res, nc.scalar)
-
-        def store(j, res, queue):
+        def store(j, res):
             a, b = divmod(j, BATCH)
             for i, out in enumerate((out_0, out_1, out_2)):
-                queue.dma_start(
+                nc.sync.dma_start(
                     out=out[b].rearrange("(p a) n -> p a n", a=GROUPS)[:, a, :],
                     in_=res[:, i * NOUT : (i + 1) * NOUT],
                 )
@@ -439,6 +439,10 @@ def tile_ffnn_encoder_pa_t_kernel(
         timing_reduce(EARLY)
         timing_cosine(EARLY)
         timing_signal(EARLY)
+        pos_late = keep.tile([P, GROUPS], F32)
+        nc.vector.tensor_copy(out=pos_late[:], in_=pos[:])
+        for a in range(EARLY + 1, GROUPS):
+            timing_whole(a, nc.gpsimd)
         embed_bias(0)
         embed_matmul(0, 0)
         embed_matmul(0, 1)
@@ -464,8 +468,6 @@ def tile_ffnn_encoder_pa_t_kernel(
                     mean_part(turn // BATCH)
             if in_range(turn - 1):
                 square_rows(turn - 1)
-            if turn % BATCH == 0 and in_range(turn - BATCH):
-                statistics(turn // BATCH - 1)
             if in_range(turn - LAG_SCALE):
                 scale_blocks(turn - LAG_SCALE)
             if in_range(turn - LAG_TRANSPOSE):
@@ -473,11 +475,13 @@ def tile_ffnn_encoder_pa_t_kernel(
             if turn in (4, 8, 12):
                 transpose_x(turn // 4)
             if in_range(turn - LAG_STORE):
-                (add_bias_apart if turn - LAG_STORE == TILES - BATCH - 2 else add_bias)(turn - LAG_STORE)
+                add_bias(turn - LAG_STORE)
             if in_range(turn - LAG_NORM) and not on_gpsimd(turn - LAG_NORM):
                 normalise(turn - LAG_NORM)
             if in_range(turn - LAG_PACK):
                 pack(turn - LAG_PACK)
+            if turn % BATCH == 0 and in_range(turn - BATCH):
+                statistics(turn // BATCH - 1)
             if turn == BATCH:
                 nc.vector.memset(w_planes[:].rearrange("p g n -> p (g n)").bitcast(I32), 0)
                 nc.vector.tensor_copy(out=affine_f[:], in_=vec_bf[:, 1:3, 0:BLOCKS])
@@ -492,8 +496,6 @@ def tile_ffnn_encoder_pa_t_kernel(
             late = range((EARLY + 1) * BATCH, TILES)
             if turn % BATCH == 1 and turn + 3 in late:
                 timing_signal((turn + 3) // BATCH)
-            if turn % BATCH == 1 and turn + 7 in late:
-                timing_whole((turn + 7) // BATCH, nc.gpsimd)
             if turn % BATCH == 2 and turn + 6 in late:
                 timing_reduce((turn + 6) // BATCH)
             if turn % BATCH == 3 and turn + 5 in late:

@@ -90,30 +90,12 @@ def tile_ffnn_encoder_pa_t_kernel(
                 in_=vec.rearrange("(g p t) -> p g t", g=PASSES, t=PACK),
             )
 
-        nc.sync.dma_start(out=x_first[:], in_=x_rows[:, :, 0:first])
         load_vector(0, b_emb)
+        nc.sync.dma_start(out=x_first[:], in_=x_rows[:, :, 0:first])
         nc.sync.dma_start(out=w_raw[:], in_=W_emb)
         nc.sync.dma_start(out=x_rest[:], in_=x_rows[:, :, first : GROUPS * FIN])
         load_vector(1, g0)
         load_vector(2, beta0)
-        one = keep.tile([P, 1], F32)
-        nc.vector.memset(one[:], 1.0)
-        freq = keep.tile([P, PACK, P], F32)
-        for t in range(PACK):
-            nc.vector.tensor_scalar(
-                out=freq[:, t, 0:1], in0=one[:], scalar1=DECAY**t / (2.0 * math.pi), scalar2=None, op0=ALU.mult
-            )
-        n = 1
-        while n < P:
-            for m in range(n, min(4 * n, P), n):
-                nc.vector.tensor_scalar(
-                    out=freq[:, :, m : m + n],
-                    in0=freq[:, :, 0:n],
-                    scalar1=DECAY ** (PACK * m),
-                    scalar2=None,
-                    op0=ALU.mult,
-                )
-            n *= 4
         zero = keep.tile([P, 1], BF16)
         nc.gpsimd.memset(zero[:], 0.0)
         for i in range(WARM_UPS):
@@ -125,14 +107,32 @@ def tile_ffnn_encoder_pa_t_kernel(
         nc.gpsimd.iota(
             pos[:], pattern=[[1, GROUPS]], base=0, channel_multiplier=GROUPS, allow_small_or_imprecise_dtypes=True
         )
+        one = keep.tile([P, 1], F32)
+        nc.vector.memset(one[:], 1.0)
+        neg_half = keep.tile([P, BATCH], F32)
+        nc.vector.memset(neg_half[:], -0.5)
+        freq = keep.tile([P, PACK, P], F32)
+        for t in range(PACK):
+            nc.vector.tensor_scalar(
+                out=freq[:, t, 0:1], in0=one[:], scalar1=DECAY**t / (2.0 * math.pi), scalar2=None, op0=ALU.mult
+            )
+        neg_rad = keep.tile([P, GROUPS], F32)
+        nc.vector.tensor_scalar(out=neg_rad[:], in0=pos[:], scalar1=-2.0 * math.pi, scalar2=None, op0=ALU.mult)
+        n = 1
+        while n < P:
+            for m in range(n, min(4 * n, P), n):
+                nc.vector.tensor_scalar(
+                    out=freq[:, :, m : m + n],
+                    in0=freq[:, :, 0:n],
+                    scalar1=DECAY ** (PACK * m),
+                    scalar2=None,
+                    op0=ALU.mult,
+                )
+            n *= 4
         ident_f = keep.tile([P, P], F32)
         make_identity(nc, ident_f[:])
         warm = keep.tile([P, 1], F32)
         nc.scalar.activation(out=warm[:], in_=one[:], func=ACT.Sin)
-        neg_rad = keep.tile([P, GROUPS], F32)
-        nc.vector.tensor_scalar(out=neg_rad[:], in0=pos[:], scalar1=-2.0 * math.pi, scalar2=None, op0=ALU.mult)
-        neg_half = keep.tile([P, BATCH], F32)
-        nc.vector.memset(neg_half[:], -0.5)
 
         w_codes = keep.tile([P, PASSES, N3], U32, align_bytes=64)
         w_planes = keep.tile([P, PASSES, N3], U8, align_bytes=64)
@@ -195,23 +195,29 @@ def tile_ffnn_encoder_pa_t_kernel(
             )
             folded_of[a] = folded
 
-        def timing_signal(a):
+        def signal_direct(a):
             signal = phase.tile([P, PASSES, PACK, P], F32, bufs=EARLY + 1)
-            turn_rad = 2.0 * math.pi
-            quarter = math.pi / 2.0
-            nc.scalar.activation(out=signal[:, 0, :, 0:WRAP], in_=reduced_of[a][:], func=ACT.Sin, scale=turn_rad)
             for g in range(PASSES):
                 nc.scalar.activation(
                     out=signal[:, g, :, WRAP:P],
                     in_=freq[:, :, WRAP:P],
                     func=ACT.Sin,
                     scale=neg_rad[:, a : a + 1],
-                    bias=(math.pi, quarter)[g],
+                    bias=(math.pi, math.pi / 2.0)[g],
                 )
-            nc.scalar.activation(
-                out=signal[:, 1, :, 0:WRAP], in_=folded_of[a][:], func=ACT.Sin, scale=-turn_rad, bias=quarter
-            )
             timing[a] = signal
+
+        def signal_wrapped(a):
+            signal = timing[a]
+            turn_rad = 2.0 * math.pi
+            nc.scalar.activation(out=signal[:, 0, :, 0:WRAP], in_=reduced_of[a][:], func=ACT.Sin, scale=turn_rad)
+            nc.scalar.activation(
+                out=signal[:, 1, :, 0:WRAP],
+                in_=folded_of[a][:],
+                func=ACT.Sin,
+                scale=-turn_rad,
+                bias=math.pi / 2.0,
+            )
 
         xT = keep.tile([P, GROUPS // PAIR, BATCH * PAIR, P], BF16)
 
@@ -420,29 +426,30 @@ def tile_ffnn_encoder_pa_t_kernel(
 
         ident_bf = keep.tile([P, P], BF16)
         nc.vector.tensor_copy(out=ident_bf[:], in_=ident_f[:])
-        for a in range(EARLY + 1):
-            timing_whole(a, nc.vector)
-        for a in range(EARLY):
-            timing_reduce(a)
+        timing_whole(0, nc.vector)
+        timing_whole(1, nc.vector)
+        timing_reduce(0)
+        timing_whole(2, nc.vector)
         timing_cosine(0)
+        timing_reduce(1)
         bias_f = keep.tile([P, BLOCKS], F32)
         nc.vector.tensor_copy(out=bias_f[:], in_=vec_bf[:, 0, 0:BLOCKS])
-        for a in range(1, EARLY):
-            timing_cosine(a)
-        timing_signal(0)
+        signal_direct(0)
+        signal_direct(1)
+        signal_wrapped(0)
         transpose_x(0)
-        nc.scalar.copy(out=xT[:, 0, :, :], in_=xt_of[0][:])
-        for a in range(1, EARLY):
-            timing_signal(a)
+        half = BATCH * PAIR // 2
+        for blocks in (slice(0, half), slice(half, 2 * half)):
+            nc.scalar.copy(out=xT[:, 0, blocks, :], in_=xt_of[0][:, blocks, :])
         w_perm = keep.tile([P, PASSES, PACK, P], BF16)
         nc.vector.tensor_copy(out=w_perm[:], in_=w_raw[:].rearrange("f (g p t) -> f g t p", g=PASSES, t=PACK))
-        timing_reduce(EARLY)
-        timing_cosine(EARLY)
-        timing_signal(EARLY)
+        timing_reduce(2)
+        timing_cosine(1)
+        timing_cosine(2)
+        signal_wrapped(1)
+        signal_direct(2)
+        signal_wrapped(2)
         pos_late = keep.tile([P, GROUPS], F32)
-        nc.vector.tensor_copy(out=pos_late[:], in_=pos[:])
-        for a in range(EARLY + 1, GROUPS):
-            timing_whole(a, nc.gpsimd)
         embed_bias(0)
         embed_matmul(0, 0)
         embed_matmul(0, 1)
@@ -459,7 +466,7 @@ def tile_ffnn_encoder_pa_t_kernel(
             if in_range(turn + 1):
                 embed_matmul(turn + 1, 1)
             if turn in (5, 9, 13):
-                nc.scalar.copy(out=xT[:, turn // 4, :, :], in_=xt_of[turn // 4][:])
+                nc.scalar.copy(out=xT[:, turn // BATCH, :, :], in_=xt_of[turn // BATCH][:])
             if in_range(turn - LAG_NORM):
                 normalise_early(turn - LAG_NORM)
             if in_range(turn):
@@ -473,7 +480,7 @@ def tile_ffnn_encoder_pa_t_kernel(
             if in_range(turn - LAG_TRANSPOSE):
                 transpose_blocks(turn - LAG_TRANSPOSE)
             if turn in (4, 8, 12):
-                transpose_x(turn // 4)
+                transpose_x(turn // BATCH)
             if in_range(turn - LAG_STORE):
                 add_bias(turn - LAG_STORE)
             if in_range(turn - LAG_NORM) and not on_gpsimd(turn - LAG_NORM):
@@ -482,7 +489,7 @@ def tile_ffnn_encoder_pa_t_kernel(
                 pack(turn - LAG_PACK)
             if turn % BATCH == 0 and in_range(turn - BATCH):
                 statistics(turn // BATCH - 1)
-            if turn == BATCH:
+            if turn == 3:
                 nc.vector.memset(w_planes[:].rearrange("p g n -> p (g n)").bitcast(I32), 0)
                 nc.vector.tensor_copy(out=affine_f[:], in_=vec_bf[:, 1:3, 0:BLOCKS])
                 for j, (words, scales, bias) in enumerate(weights):
@@ -493,9 +500,14 @@ def tile_ffnn_encoder_pa_t_kernel(
                         )
                 for j, (words, scales, bias) in enumerate(weights):
                     nc.sync.dma_start(out=bias_bc[:, j * NOUT : (j + 1) * NOUT], in_=bias.partition_broadcast(P))
+            if turn == 0:
+                nc.vector.tensor_copy(out=pos_late[:], in_=pos[:])
+                for a in range(EARLY + 1, GROUPS):
+                    timing_whole(a, nc.gpsimd)
             late = range((EARLY + 1) * BATCH, TILES)
             if turn % BATCH == 1 and turn + 3 in late:
-                timing_signal((turn + 3) // BATCH)
+                signal_direct((turn + 3) // BATCH)
+                signal_wrapped((turn + 3) // BATCH)
             if turn % BATCH == 2 and turn + 6 in late:
                 timing_reduce((turn + 6) // BATCH)
             if turn % BATCH == 3 and turn + 5 in late:

@@ -370,7 +370,7 @@ def tile_ffnn_encoder_pa_t_kernel(
                 grouped = cols.tile([P, BATCH * P, PACK], BF16, align_bytes=64)
                 mine = BATCH * P
                 if m + LAG_PACK >= TILES + LAG_NORM:
-                    mine -= (2 if m == TILES - 2 else 1) * P
+                    mine -= (3 if m == TILES - 2 else 1) * P
                 nc.vector.tensor_copy(
                     out=grouped[:, 0:mine, :].rearrange("p (c i) t -> p c t i", i=4),
                     in_=ht_of[a, g][:, :, 0:mine].rearrange("p t (c i) -> p c t i", i=4),
@@ -461,10 +461,10 @@ def tile_ffnn_encoder_pa_t_kernel(
             if in_range(turn + 1):
                 embed_bias(turn + 1)
                 embed_matmul(turn + 1, 0)
-            if in_range(turn - LAG_PROJECT):
-                project_matmuls(turn - LAG_PROJECT)
             if in_range(turn + 1):
                 embed_matmul(turn + 1, 1)
+            if in_range(turn - LAG_PROJECT):
+                project_matmuls(turn - LAG_PROJECT)
             if turn in (5, 9, 13):
                 nc.scalar.copy(out=xT[:, turn // BATCH, :, :], in_=xt_of[turn // BATCH][:])
             if in_range(turn - LAG_NORM):

import math
from contextlib import ExitStack

import concourse.mybir as mybir
from concourse.masks import make_identity

F32 = mybir.dt.float32
BF16 = mybir.dt.bfloat16
I32 = mybir.dt.int32
U32 = mybir.dt.uint32
U8 = mybir.dt.uint8
FP8X4 = mybir.dt.float8_e4m3fn_x4
ALU = mybir.AluOpType
ACT = mybir.ActivationFunctionType

P = 128
BATCH = 4
SEQ = 1024
FIN = 128
D = 1024
NOUT = 256
N3 = 3 * NOUT
PACK = 4
PASSES = D // (P * PACK)
HALF = P * PACK
BLOCKS = PASSES * PACK
GROUPS = SEQ // P
TILES = GROUPS * BATCH
PAIR = 2
EPS = 1e-3
DECAY = math.exp(-math.log(10000.0) / 511.0)
FIRST_SMALL = math.ceil(511.0 * math.log((SEQ - 1) / (1.5 * math.pi)) / math.log(10000.0))
WRAP = -(-FIRST_SMALL // PACK)

WARM_UPS = 4
EARLY = 2

LAG_NORM = 5
LAG_TRANSPOSE = 9
LAG_SCALE = 10
LAG_PACK = 12
LAG_PROJECT = 16
LAG_STORE = 17

FLOPS = 2 * BATCH * SEQ * FIN * D + 2 * BATCH * SEQ * D * N3


def tile_ffnn_encoder_pa_t_kernel(
    tc,
    x,
    W_emb,
    b_emb,
    g0,
    beta0,
    Wq_words,
    Wq_scales,
    bq,
    Wk_words,
    Wk_scales,
    bk,
    Wv_words,
    Wv_scales,
    bv,
    out_0,
    out_1,
    out_2,
):
    nc = tc.nc
    with ExitStack() as stack:
        keep = stack.enter_context(tc.tile_pool(name="keep", bufs=1))
        phase = stack.enter_context(tc.tile_pool(name="phase", bufs=2))
        rows = stack.enter_context(tc.tile_pool(name="rows", bufs=3))
        small = stack.enter_context(tc.tile_pool(name="small", bufs=3))
        cols = stack.enter_context(tc.tile_pool(name="cols", bufs=2))
        results = stack.enter_context(tc.tile_pool(name="results", bufs=6))
        psum_z = stack.enter_context(tc.psum_pool(name="psum_z", bufs=5))
        psum_t = stack.enter_context(tc.psum_pool(name="psum_t", bufs=3))
        stack.enter_context(tc.manual_schedule())

        first = PAIR * FIN
        x_first = keep.tile([P, BATCH, first], BF16)
        x_rest = keep.tile([P, BATCH, GROUPS * FIN - first], BF16)
        w_raw = keep.tile([P, D], BF16)
        x_rows = x.rearrange("b (p a) f -> p b (a f)", a=GROUPS)
        vec_bf = keep.tile([P, 3, 16], BF16)

        def load_vector(i, vec):
            nc.sync.dma_start(
                out=vec_bf[:, i, 0:BLOCKS].rearrange("p (g t) -> p g t", t=PACK),
                in_=vec.rearrange("(g p t) -> p g t", g=PASSES, t=PACK),
            )

        load_vector(0, b_emb)
        nc.sync.dma_start(out=x_first[:], in_=x_rows[:, :, 0:first])
        nc.sync.dma_start(out=w_raw[:], in_=W_emb)
        nc.sync.dma_start(out=x_rest[:], in_=x_rows[:, :, first : GROUPS * FIN])
        load_vector(1, g0)
        load_vector(2, beta0)
        zero = keep.tile([P, 1], BF16)
        nc.gpsimd.memset(zero[:], 0.0)
        for i in range(WARM_UPS):
            idle = psum_z.tile([P, HALF], F32, tag="z")
            nc.tensor.matmul(
                out=idle[:], lhsT=zero[:].to_broadcast([P, P]), rhs=zero[:].to_broadcast([P, HALF]), start=True, stop=True
            )
        pos = keep.tile([P, GROUPS], F32)
        nc.gpsimd.iota(
            pos[:], pattern=[[1, GROUPS]], base=0, channel_multiplier=GROUPS, allow_small_or_imprecise_dtypes=True
        )
        one = keep.tile([P, 1], F32)
        nc.vector.memset(one[:], 1.0)
        neg_half = keep.tile([P, BATCH], F32)
        nc.vector.memset(neg_half[:], -0.5)
        freq = keep.tile([P, PACK, P], F32)
        for t in range(PACK):
            nc.vector.tensor_scalar(
                out=freq[:, t, 0:1], in0=one[:], scalar1=DECAY**t / (2.0 * math.pi), scalar2=None, op0=ALU.mult
            )
        neg_rad = keep.tile([P, GROUPS], F32)
        nc.vector.tensor_scalar(out=neg_rad[:], in0=pos[:], scalar1=-2.0 * math.pi, scalar2=None, op0=ALU.mult)
        n = 1
        while n < P:
            for m in range(n, min(4 * n, P), n):
                nc.vector.tensor_scalar(
                    out=freq[:, :, m : m + n],
                    in0=freq[:, :, 0:n],
                    scalar1=DECAY ** (PACK * m),
                    scalar2=None,
                    op0=ALU.mult,
                )
            n *= 4
        ident_f = keep.tile([P, P], F32)
        make_identity(nc, ident_f[:])
        warm = keep.tile([P, 1], F32)
        nc.scalar.activation(out=warm[:], in_=one[:], func=ACT.Sin)

        w_codes = keep.tile([P, PASSES, N3], U32, align_bytes=64)
        w_planes = keep.tile([P, PASSES, N3], U8, align_bytes=64)
        weights = ((Wq_words, Wq_scales, bq), (Wk_words, Wk_scales, bk), (Wv_words, Wv_scales, bv))
        for j, (words, scales, bias) in enumerate(weights):
            nc.sync.dma_start(
                out=w_codes[:, :, j * NOUT : (j + 1) * NOUT].bitcast(I32),
                in_=words.rearrange("g p n t -> p g (n t)").bitcast(I32),
            )

        xt_of = {}
        whole_of = {}
        reduced_of = {}
        folded_of = {}
        mean_of = {}
        timing = {}
        z_of = {}
        e_of = {}
        sum_of = {}
        sq_of = {}
        scale_of = {}
        shift_of = {}
        n_of = {}
        nt_of = {}
        ht_of = {}
        grouped_of = {}
        codes_of = {}
        planes_of = {}
        acc_of = {}

        def timing_whole(a, engine):
            whole = phase.tile([P, PACK, WRAP], I32, bufs=GROUPS)
            engine.tensor_scalar(
                out=whole[:],
                in0=freq[:, :, 0:WRAP],
                scalar1=(pos_late if a > EARLY else pos)[:, a : a + 1],
                scalar2=0.0,
                op0=ALU.mult,
                op1=ALU.add,
            )
            whole_of[a] = whole

        def timing_reduce(a):
            reduced = phase.tile([P, PACK, WRAP], F32, bufs=EARLY + 1)
            nc.vector.scalar_tensor_tensor(
                out=reduced[:],
                in0=freq[:, :, 0:WRAP],
                scalar=pos[:, a : a + 1],
                in1=whole_of[a][:],
                op0=ALU.mult,
                op1=ALU.subtract,
            )
            reduced_of[a] = reduced

        def timing_cosine(a):
            reduced = reduced_of[a]
            folded = phase.tile([P, PACK, WRAP], F32, bufs=EARLY + 1)
            nc.vector.scalar_tensor_tensor(
                out=folded[:], in0=reduced[:], scalar=0.25, in1=reduced[:], op0=ALU.is_gt, op1=ALU.subtract
            )
            folded_of[a] = folded

        def signal_direct(a):
            signal = phase.tile([P, PASSES, PACK, P], F32, bufs=EARLY + 1)
            for g in range(PASSES):
                nc.scalar.activation(
                    out=signal[:, g, :, WRAP:P],
                    in_=freq[:, :, WRAP:P],
                    func=ACT.Sin,
                    scale=neg_rad[:, a : a + 1],
                    bias=(math.pi, math.pi / 2.0)[g],
                )
            timing[a] = signal

        def signal_wrapped(a):
            signal = timing[a]
            turn_rad = 2.0 * math.pi
            nc.scalar.activation(out=signal[:, 0, :, 0:WRAP], in_=reduced_of[a][:], func=ACT.Sin, scale=turn_rad)
            nc.scalar.activation(
                out=signal[:, 1, :, 0:WRAP],
                in_=folded_of[a][:],
                func=ACT.Sin,
                scale=-turn_rad,
                bias=math.pi / 2.0,
            )

        xT = keep.tile([P, GROUPS // PAIR, BATCH * PAIR, P], BF16)

        def transpose_x(q):
            xt_ps = psum_z.tile([P, BATCH * PAIR, P], BF16, tag="z")
            for b in range(BATCH):
                for a in range(PAIR):
                    rows_x = x_first[:, b, :] if q == 0 else x_rest[:, b, (q - 1) * first : q * first]
                    nc.tensor.transpose(xt_ps[:, b * PAIR + a, :], rows_x[:, a * FIN : (a + 1) * FIN], ident_bf[:])
            xt_of[q] = xt_ps

        def embed_bias(j):
            banks = []
            for g in range(PASSES):
                z = psum_z.tile([P, HALF], F32, tag="z")
                for t in range(PACK):
                    c = g * PACK + t
                    nc.tensor.matmul(
                        out=z[:, t * P : (t + 1) * P],
                        lhsT=bias_f[:, c : c + 1].to_broadcast([P, P]),
                        rhs=ident_f[:],
                        is_transpose=True,
                        start=(t == 0),
                        stop=False,
                    )
                banks.append(z)
            z_of[j] = banks

        def embed_matmul(j, g):
            a, b = divmod(j, BATCH)
            nc.tensor.matmul(
                out=z_of[j][g][:],
                lhsT=xT[:, a // PAIR, b * PAIR + a % PAIR, :],
                rhs=w_perm[:, g, :, :].rearrange("f t p -> f (t p)"),
                start=False,
                stop=True,
            )

        def embed_rows(j):
            a, b = divmod(j, BATCH)
            if b == 0:
                e_of[a] = rows.tile([P, BATCH, D], F32, name="e")
                sum_of[a] = small.tile([P, BATCH, PASSES], F32, name="sum_e")
                sq_of[a] = small.tile([P, BATCH], F32, name="sum_sq")
            for g in range(PASSES):
                nc.vector.scalar_tensor_tensor(
                    out=e_of[a][:, b, g * HALF : (g + 1) * HALF],
                    in0=z_of[j][g][:],
                    scalar=0.0,
                    in1=timing[a][:, g, :, :].rearrange("p t c -> p (t c)"),
                    op0=ALU.max,
                    op1=ALU.add,
                    accum_out=sum_of[a][:, b, g : g + 1],
                )

        def square_rows(j):
            a, b = divmod(j, BATCH)
            squares = cols.tile([P, D], BF16)
            nc.scalar.activation(
                out=squares[:],
                in_=e_of[a][:, b, :],
                func=ACT.Square,
                scale=1.0 / math.sqrt(D),
                accum_out=sq_of[a][:, b : b + 1],
            )

        def mean_part(a):
            neg_mean = small.tile([P, BATCH], F32)
            nc.gpsimd.tensor_tensor(out=neg_mean[:], in0=sum_of[a][:, :, 0], in1=sum_of[a][:, :, 1], op=ALU.add)
            nc.gpsimd.tensor_scalar(
                out=neg_mean[:], in0=neg_mean[:], scalar1=-1.0 / D, scalar2=0.0, op0=ALU.mult, op1=ALU.add
            )
            rest = small.tile([P, BATCH], F32)
            nc.gpsimd.tensor_tensor(out=rest[:], in0=neg_mean[:], in1=neg_mean[:], op=ALU.mult)
            nc.gpsimd.tensor_scalar(out=rest[:], in0=rest[:], scalar1=-1.0, scalar2=EPS, op0=ALU.mult, op1=ALU.add)
            mean_of[a] = (neg_mean, rest)

        def statistics(a):
            neg_mean, rest = mean_of[a]
            var = small.tile([P, BATCH], F32)
            nc.vector.tensor_tensor(out=var[:], in0=sq_of[a][:], in1=rest[:], op=ALU.add)
            rstd = small.tile([P, BATCH], F32)
            nc.gpsimd.tensor_tensor(out=rstd[:], in0=var[:], in1=neg_half[:], op=ALU.pow)
            shift = small.tile([P, BATCH], F32)
            nc.gpsimd.tensor_tensor(out=shift[:], in0=neg_mean[:], in1=rstd[:], op=ALU.mult)
            scale_of[a] = rstd
            shift_of[a] = shift

        def on_gpsimd(j):
            a, b = divmod(j, BATCH)
            return 1 < j < TILES - BATCH and b in (1, 2)

        def normalise_early(j):
            a, b = divmod(j, BATCH)
            if b == 0:
                n_of[a] = rows.tile([P, BATCH, D], F32, name="normed")
            if on_gpsimd(j):
                gate = small.tile([P, 1], F32)
                nc.vector.tensor_copy(out=gate[:], in_=shift_of[a][:, b : b + 1])
                nc.gpsimd.tensor_scalar(
                    out=n_of[a][:, b, :],
                    in0=e_of[a][:, b, :],
                    scalar1=scale_of[a][:, b : b + 1],
                    scalar2=gate[:],
                    op0=ALU.mult,
                    op1=ALU.add,
                )

        def normalise(j):
            a, b = divmod(j, BATCH)
            rows_in, rows_out = e_of[a][:, b, :], n_of[a][:, b, :]
            scale, shift = scale_of[a][:, b : b + 1], shift_of[a][:, b : b + 1]
            filling = j + LAG_NORM < LAG_PROJECT
            if (filling and b == 0) or j in (BATCH - 1, TILES - BATCH):
                nc.vector.tensor_scalar(
                    out=rows_out, in0=rows_in, scalar1=scale, scalar2=shift, op0=ALU.mult, op1=ALU.add
                )
            else:
                nc.scalar.activation(out=rows_out, in_=rows_in, func=ACT.Identity, scale=scale, bias=shift)

        def transpose_blocks(k):
            a, quarter = divmod(k, BATCH)
            for c in (2 * quarter, 2 * quarter + 1):
                nt = psum_t.tile([P, BATCH, P], F32)
                for b in range(BATCH):
                    nc.tensor.transpose(nt[:, b, :], n_of[a][:, b, c * P : (c + 1) * P], ident_f[:])
                nt_of[a, c] = nt

        def scale_blocks(k):
            a, quarter = divmod(k, BATCH)
            for c in (2 * quarter, 2 * quarter + 1):
                g, t = divmod(c, PACK)
                if t == 0:
                    ht_of[a, g] = cols.tile([P, PACK, BATCH * P], BF16, name="ht")
                nc.scalar.activation(
                    out=ht_of[a, g][:, t, :],
                    in_=nt_of[a, c][:].rearrange("p b k -> p (b k)"),
                    func=ACT.Identity,
                    scale=affine_f[:, 0, c : c + 1],
                    bias=affine_f[:, 1, c : c + 1],
                )

        def pack(m):
            a, piece = divmod(m, BATCH)
            g, quantise = divmod(piece, 2)
            if piece == 0:
                codes_of[a] = cols.tile([P, PASSES, BATCH * P], U32, name="codes", align_bytes=64)
                planes_of[a] = cols.tile([P, PASSES, BATCH * P], U8, name="planes", align_bytes=64)
            if not quantise:
                grouped = cols.tile([P, BATCH * P, PACK], BF16, align_bytes=64)
                mine = BATCH * P
                if m + LAG_PACK >= TILES + LAG_NORM:
                    mine -= (3 if m == TILES - 2 else 1) * P
                nc.vector.tensor_copy(
                    out=grouped[:, 0:mine, :].rearrange("p (c i) t -> p c t i", i=4),
                    in_=ht_of[a, g][:, :, 0:mine].rearrange("p t (c i) -> p c t i", i=4),
                )
                if mine < BATCH * P:
                    nc.scalar.copy(
                        out=grouped[:, mine : BATCH * P, :].rearrange("p (c i) t -> p c t i", i=4),
                        in_=ht_of[a, g][:, :, mine : BATCH * P].rearrange("p t (c i) -> p c t i", i=4),
                    )
                grouped_of[a, g] = grouped
            else:
                nc.vector.quantize_mx(
                    out=codes_of[a][:, g, :].bitcast(FP8X4),
                    scales=planes_of[a][:, g, :],
                    in_=grouped_of[a, g][:].rearrange("p k t -> p (k t)"),
                )

        def project_matmuls(j):
            a, b = divmod(j, BATCH)
            tok = slice(b * P, (b + 1) * P)
            acc_qk = psum_z.tile([P, 2 * NOUT], F32, tag="z")
            acc_v = psum_z.tile([P, NOUT], F32, tag="z")
            for acc, n_cols in ((acc_qk, slice(0, 2 * NOUT)), (acc_v, slice(2 * NOUT, N3))):
                for g in range(PASSES):
                    nc.tensor.matmul_mx(
                        out=acc[:],
                        lhsT=codes_of[a][:, g, tok].bitcast(FP8X4),
                        lhsT_scale=planes_of[a][:, g, tok],
                        rhs=w_codes[:, g, n_cols].bitcast(FP8X4),
                        rhs_scale=w_planes[:, g, n_cols],
                        start=(g == 0),
                        stop=(g == PASSES - 1),
                    )
            acc_of[j] = (acc_qk, acc_v)

        def add_bias(j):
            acc_qk, acc_v = acc_of[j]
            res = results.tile([P, N3], F32)
            for acc, n_cols in ((acc_qk, slice(0, 2 * NOUT)), (acc_v, slice(2 * NOUT, N3))):
                nc.vector.tensor_tensor(out=res[:, n_cols], in0=acc[:], in1=bias_bc[:, n_cols], op=ALU.add)
            store(j, res)

        def store(j, res):
            a, b = divmod(j, BATCH)
            for i, out in enumerate((out_0, out_1, out_2)):
                nc.sync.dma_start(
                    out=out[b].rearrange("(p a) n -> p a n", a=GROUPS)[:, a, :],
                    in_=res[:, i * NOUT : (i + 1) * NOUT],
                )

        def in_range(j):
            return 0 <= j < TILES

        ident_bf = keep.tile([P, P], BF16)
        nc.vector.tensor_copy(out=ident_bf[:], in_=ident_f[:])
        timing_whole(0, nc.vector)
        timing_whole(1, nc.vector)
        timing_reduce(0)
        timing_whole(2, nc.vector)
        timing_cosine(0)
        timing_reduce(1)
        bias_f = keep.tile([P, BLOCKS], F32)
        nc.vector.tensor_copy(out=bias_f[:], in_=vec_bf[:, 0, 0:BLOCKS])
        signal_direct(0)
        signal_direct(1)
        signal_wrapped(0)
        transpose_x(0)
        half = BATCH * PAIR // 2
        for blocks in (slice(0, half), slice(half, 2 * half)):
            nc.scalar.copy(out=xT[:, 0, blocks, :], in_=xt_of[0][:, blocks, :])
        w_perm = keep.tile([P, PASSES, PACK, P], BF16)
        nc.vector.tensor_copy(out=w_perm[:], in_=w_raw[:].rearrange("f (g p t) -> f g t p", g=PASSES, t=PACK))
        timing_reduce(2)
        timing_cosine(1)
        timing_cosine(2)
        signal_wrapped(1)
        signal_direct(2)
        signal_wrapped(2)
        pos_late = keep.tile([P, GROUPS], F32)
        embed_bias(0)
        embed_matmul(0, 0)
        embed_matmul(0, 1)
        affine_f = keep.tile([P, 2, BLOCKS], F32)

        bias_bc = keep.tile([P, N3], BF16)

        for turn in range(TILES + LAG_STORE):
            if in_range(turn + 1):
                embed_bias(turn + 1)
                embed_matmul(turn + 1, 0)
            if in_range(turn + 1):
                embed_matmul(turn + 1, 1)
            if in_range(turn - LAG_PROJECT):
                project_matmuls(turn - LAG_PROJECT)
            if turn in (5, 9, 13):
                nc.scalar.copy(out=xT[:, turn // BATCH, :, :], in_=xt_of[turn // BATCH][:])
            if in_range(turn - LAG_NORM):
                normalise_early(turn - LAG_NORM)
            if in_range(turn):
                embed_rows(turn)
                if turn % BATCH == BATCH - 1:
                    mean_part(turn // BATCH)
            if in_range(turn - 1):
                square_rows(turn - 1)
            if in_range(turn - LAG_SCALE):
                scale_blocks(turn - LAG_SCALE)
            if in_range(turn - LAG_TRANSPOSE):
                transpose_blocks(turn - LAG_TRANSPOSE)
            if turn in (4, 8, 12):
                transpose_x(turn // BATCH)
            if in_range(turn - LAG_STORE):
                add_bias(turn - LAG_STORE)
            if in_range(turn - LAG_NORM) and not on_gpsimd(turn - LAG_NORM):
                normalise(turn - LAG_NORM)
            if in_range(turn - LAG_PACK):
                pack(turn - LAG_PACK)
            if turn % BATCH == 0 and in_range(turn - BATCH):
                statistics(turn // BATCH - 1)
            if turn == 3:
                nc.vector.memset(w_planes[:].rearrange("p g n -> p (g n)").bitcast(I32), 0)
                nc.vector.tensor_copy(out=affine_f[:], in_=vec_bf[:, 1:3, 0:BLOCKS])
                for j, (words, scales, bias) in enumerate(weights):
                    for quad in range(4):
                        nc.sync.dma_start(
                            out=w_planes[32 * quad : 32 * quad + 4, :, j * NOUT : (j + 1) * NOUT].bitcast(I32),
                            in_=scales.bitcast(I32)[:, 4 * quad : 4 * quad + 4, :].rearrange("g r n -> r g n"),
                        )
                for j, (words, scales, bias) in enumerate(weights):
                    nc.sync.dma_start(out=bias_bc[:, j * NOUT : (j + 1) * NOUT], in_=bias.partition_broadcast(P))
            if turn == 0:
                nc.vector.tensor_copy(out=pos_late[:], in_=pos[:])
                for a in range(EARLY + 1, GROUPS):
                    timing_whole(a, nc.gpsimd)
            late = range((EARLY + 1) * BATCH, TILES)
            if turn % BATCH == 1 and turn + 3 in late:
                signal_direct((turn + 3) // BATCH)
                signal_wrapped((turn + 3) // BATCH)
            if turn % BATCH == 2 and turn + 6 in late:
                timing_reduce((turn + 6) // BATCH)
            if turn % BATCH == 3 and turn + 5 in late:
                timing_cosine((turn + 5) // BATCH)
